import numpy as np
import ml_dtypes


def mxq(x, axis, fmt="e4m3"):
    dtype, down = {"e4m3": (ml_dtypes.float8_e4m3fn, 7), "e5m2": (ml_dtypes.float8_e5m2, 14)}[fmt]
    v = np.moveaxis(np.asarray(x, np.float32).astype(ml_dtypes.bfloat16).astype(np.float64), axis, -1)
    blocks = v.reshape(v.shape[:-1] + (-1, 32))
    amax = np.abs(blocks).max(-1, keepdims=True)
    byte = np.maximum(np.where(amax > 0, np.frexp(amax)[1] - 1 + 127, 0) - down, 1)
    scale = np.exp2(byte - 127.0)
    codes = (blocks / scale).astype(np.float32).astype(dtype).astype(np.float64)
    return np.moveaxis((codes * scale).reshape(v.shape), -1, axis)


WIDE = False


def mx_kscale(k):
    if not WIDE:
        return np.ones(k)
    levels = np.array([10, -10, 5, -5, 0])
    a = np.random.permutation(np.resize(levels, k // 512 * 4)).reshape(k // 512, 4)
    idx = np.arange(k)
    return np.exp2(a[idx // 512, idx % 128 // 32])


BF16 = ml_dtypes.bfloat16


def bf(x):
    return np.asarray(x, np.float32).astype(BF16)


def f64(x):
    return np.asarray(x).astype(np.float64)


B, C, CQ, N = 16, 512, 128, 512
EPS = 1e-6
LEAKY_SLOPE = 0.2


def setup_inputs():
    s = mx_kscale(C)
    u = s / s.max()
    sf = np.sqrt(1.5) / CQ ** 0.25
    return {
        "x": bf(np.random.standard_normal((B, C, N)) * 0.5 * u[:, None]),
        "f": bf(np.random.standard_normal((B, CQ, N)) * sf),
        "g": bf(np.random.standard_normal((B, CQ, N)) * sf),
        "mask": bf(np.random.uniform(size=(B, N))),
        "Wv": bf(np.random.standard_normal((C, C)) * 8.0 / np.sqrt(C) / u),
        "gamma": bf(1.25 + 0.1 * np.random.standard_normal(1)),
    }


def reference(x, f, g, mask, Wv, gamma):
    xf = f64(x)
    m = f64(mask)
    h = mxq(f64(Wv), 1, "e4m3") @ mxq(xf, 1, "e4m3")
    scores = f64(f).transpose(0, 2, 1) @ f64(g)
    scores = np.where(scores >= 0, scores, LEAKY_SLOPE * scores)
    e = np.exp(scores - scores.max(axis=1, keepdims=True))
    beta = e / e.sum(axis=1, keepdims=True)
    beta = beta * m[:, :, None]
    beta = beta / (beta.sum(axis=1, keepdims=True) + EPS)
    o = mxq(h, 2, "e4m3") @ mxq(beta, 1, "e4m3")
    return f64(gamma)[0] * o * m[:, None, :] + xf

@@ -1,0 +1,205 @@
+from contextlib import ExitStack
+
+import concourse.mybir as mybir
+from concourse.masks import make_identity
+
+F32 = mybir.dt.float32
+BF16 = mybir.dt.bfloat16
+U32 = mybir.dt.uint32
+U8 = mybir.dt.uint8
+FP8X4 = mybir.dt.float8_e4m3fn_x4
+ALU = mybir.AluOpType
+ACT = mybir.ActivationFunctionType
+
+B, C, CQ, N = 16, 512, 128, 512
+P = 128
+PACK = 4
+EPS = 1e-6
+LEAKY_SLOPE = 0.2
+
+FLOPS = B * (2 * C * C * N + 2 * CQ * N * N + 2 * C * N * N)
+
+
+def quantise(nc, grouped, codes, scales):
+    nc.vector.quantize_mx(
+        out=codes[:].bitcast(FP8X4),
+        scales=scales[:],
+        in_=grouped[:].rearrange("p w t -> p (w t)"),
+    )
+
+
+def tile_transformer_pa_t_kernel(tc, x, f, g, mask, Wv, gamma, out):
+    nc = tc.nc
+    with ExitStack() as stack:
+        const = stack.enter_context(tc.tile_pool(name="const", bufs=1))
+        loads = stack.enter_context(tc.tile_pool(name="loads", bufs=3))
+        work = stack.enter_context(tc.tile_pool(name="work", bufs=2))
+        stats = stack.enter_context(tc.tile_pool(name="stats", bufs=2))
+        psum = stack.enter_context(tc.psum_pool(name="psum", bufs=2))
+
+        identity = const.tile([P, P], BF16)
+        make_identity(nc, identity[:])
+
+        w_rows = const.tile([P, PACK, C], BF16)
+        nc.sync.dma_start(out=w_rows[:], in_=Wv.rearrange("(u p) c -> p u c", p=P))
+
+        gamma_bf = const.tile([P, 1], BF16)
+        nc.sync.dma_start(out=gamma_bf[:], in_=gamma.partition_broadcast(P))
+        gamma_col = const.tile([P, 1], F32)
+        nc.vector.tensor_copy(out=gamma_col[:], in_=gamma_bf[:])
+
+        mask_rows = const.tile([P, B, N], BF16)
+        for b in range(B):
+            nc.gpsimd.dma_start(out=mask_rows[:, b, :], in_=mask[b].partition_broadcast(P))
+
+        w_grouped = const.tile([P, C, PACK], BF16, align_bytes=64)
+        for u in range(PACK):
+            w_t = psum.tile([P, PACK, P], BF16, tag="transposed")
+            for t in range(PACK):
+                nc.tensor.transpose(w_t[:, t, :], w_rows[:, u, t * P : (t + 1) * P], identity[:])
+            nc.vector.tensor_copy(
+                out=w_grouped[:, u * P : (u + 1) * P, :], in_=w_t[:].rearrange("p t o -> p o t")
+            )
+        w_codes = const.tile([P, C], U32, align_bytes=64)
+        w_scales = const.tile([P, C], U8, align_bytes=64)
+        quantise(nc, w_grouped, w_codes, w_scales)
+
+        for b in range(B):
+            x_rows = loads.tile([P, PACK, N], BF16, bufs=4)
+            nc.sync.dma_start(out=x_rows[:], in_=x[b].rearrange("(t p) n -> p t n", p=P))
+            f_sb = loads.tile([P, N], BF16)
+            nc.sync.dma_start(out=f_sb[:], in_=f[b])
+            g_sb = loads.tile([P, N], BF16)
+            nc.sync.dma_start(out=g_sb[:], in_=g[b])
+
+            x_grouped = work.tile([P, N, PACK], BF16, align_bytes=64)
+            nc.scalar.copy(
+                out=x_grouped[:].rearrange("p (c i) t -> p c t i", i=4),
+                in_=x_rows[:].rearrange("p t (c i) -> p c t i", i=4),
+            )
+            x_codes = work.tile([P, N], U32, align_bytes=64)
+            x_scales = work.tile([P, N], U8, align_bytes=64)
+            quantise(nc, x_grouped, x_codes, x_scales)
+
+            h_grouped = work.tile([P, C, PACK], BF16, align_bytes=64)
+            for u in range(PACK):
+                h_ps = psum.tile([P, PACK, P], F32, tag="h")
+                for t in range(PACK):
+                    nc.tensor.matmul_mx(
+                        out=h_ps[:, t, :],
+                        lhsT=x_codes[:, t * P : (t + 1) * P].bitcast(FP8X4),
+                        lhsT_scale=x_scales[:, t * P : (t + 1) * P],
+                        rhs=w_codes[:, u * P : (u + 1) * P].bitcast(FP8X4),
+                        rhs_scale=w_scales[:, u * P : (u + 1) * P],
+                        start=True,
+                        stop=True,
+                    )
+                nc.scalar.copy(
+                    out=h_grouped[:, u * P : (u + 1) * P, :], in_=h_ps[:].rearrange("p t o -> p o t")
+                )
+            h_codes = work.tile([P, C], U32, align_bytes=64)
+            h_scales = work.tile([P, C], U8, align_bytes=64)
+            quantise(nc, h_grouped, h_codes, h_scales)
+
+            s_sb = work.tile([P, PACK, N], F32)
+            s_max = stats.tile([P, PACK], F32)
+            for v in range(PACK):
+                s_ps = psum.tile([P, N], F32, tag="s")
+                nc.tensor.matmul(
+                    out=s_ps[:], lhsT=g_sb[:, v * P : (v + 1) * P], rhs=f_sb[:], start=True, stop=True
+                )
+                nc.vector.tensor_scalar(
+                    out=s_sb[:, v, :],
+                    in0=s_ps[:],
+                    scalar1=1.0,
+                    scalar2=None,
+                    op0=ALU.mult,
+                    op1=ALU.max,
+                    accum_out=s_max[:, v : v + 1],
+                )
+            neg_slope_max = stats.tile([P, PACK], F32)
+            nc.vector.tensor_scalar(
+                out=neg_slope_max[:], in0=s_max[:], scalar1=-LEAKY_SLOPE, scalar2=None, op0=ALU.mult
+            )
+            neg_max = stats.tile([P, PACK], F32)
+            nc.vector.scalar_tensor_tensor(
+                out=neg_max[:], in0=s_max[:], scalar=-1.0, in1=neg_slope_max[:], op0=ALU.mult, op1=ALU.min
+            )
+            leaky = work.tile([P, PACK, N], F32)
+            nc.vector.scalar_tensor_tensor(
+                out=leaky[:].rearrange("p v i -> p (v i)"),
+                in0=s_sb[:].rearrange("p v i -> p (v i)"),
+                scalar=LEAKY_SLOPE,
+                in1=s_sb[:].rearrange("p v i -> p (v i)"),
+                op0=ALU.mult,
+                op1=ALU.max,
+            )
+
+            e_sb = work.tile([P, PACK, N], F32)
+            e_sum = stats.tile([P, PACK], F32)
+            em_sb = work.tile([P, PACK, N], F32)
+            em_sum = stats.tile([P, PACK], F32)
+            for v in range(PACK):
+                nc.scalar.activation(
+                    out=e_sb[:, v, :],
+                    in_=leaky[:, v, :],
+                    func=ACT.Exp,
+                    bias=neg_max[:, v : v + 1],
+                    scale=1.0,
+                    accum_out=e_sum[:, v : v + 1],
+                )
+                nc.vector.scalar_tensor_tensor(
+                    out=em_sb[:, v, :],
+                    in0=e_sb[:, v, :],
+                    scalar=1.0,
+                    in1=mask_rows[:, b, :],
+                    op0=ALU.mult,
+                    op1=ALU.mult,
+                    accum_out=em_sum[:, v : v + 1],
+                )
+            denom = stats.tile([P, PACK], F32)
+            nc.vector.scalar_tensor_tensor(
+                out=denom[:], in0=e_sum[:], scalar=EPS, in1=em_sum[:], op0=ALU.mult, op1=ALU.add
+            )
+            recip = stats.tile([P, PACK], F32)
+            nc.vector.reciprocal(out=recip[:], in_=denom[:])
+
+            beta_t = work.tile([P, PACK, N], BF16)
+            beta_grouped = work.tile([P, N, PACK], BF16, align_bytes=64)
+            for v in range(PACK):
+                nc.scalar.activation(
+                    out=beta_t[:, v, :], in_=em_sb[:, v, :], func=ACT.Copy, scale=recip[:, v : v + 1]
+                )
+                beta_ps = psum.tile([P, PACK, P], BF16, tag="transposed")
+                for t in range(PACK):
+                    nc.tensor.transpose(beta_ps[:, t, :], beta_t[:, v, t * P : (t + 1) * P], identity[:])
+                nc.scalar.copy(
+                    out=beta_grouped[:, v * P : (v + 1) * P, :], in_=beta_ps[:].rearrange("p t j -> p j t")
+                )
+            beta_codes = work.tile([P, N], U32, align_bytes=64)
+            beta_scales = work.tile([P, N], U8, align_bytes=64)
+            quantise(nc, beta_grouped, beta_codes, beta_scales)
+
+            scaled = work.tile([P, PACK, N], F32)
+            for u in range(PACK):
+                o_ps = psum.tile([P, N], F32, tag="o")
+                nc.tensor.matmul_mx(
+                    out=o_ps[:],
+                    lhsT=h_codes[:, u * P : (u + 1) * P].bitcast(FP8X4),
+                    lhsT_scale=h_scales[:, u * P : (u + 1) * P],
+                    rhs=beta_codes[:].bitcast(FP8X4),
+                    rhs_scale=beta_scales[:],
+                    start=True,
+                    stop=True,
+                )
+                nc.vector.scalar_tensor_tensor(
+                    out=scaled[:, u, :],
+                    in0=o_ps[:],
+                    scalar=gamma_col[:, 0:1],
+                    in1=mask_rows[:, b, :],
+                    op0=ALU.mult,
+                    op1=ALU.mult,
+                )
+            result = work.tile([P, PACK, N], F32)
+            nc.gpsimd.tensor_tensor(out=result[:], in0=scaled[:], in1=x_rows[:], op=ALU.add)
+            nc.gpsimd.dma_start(out=out[b].rearrange("(u p) n -> p u n", p=P), in_=result[:])

@@ -201,5 +201,5 @@ def tile_transformer_pa_t_kernel(tc, x, f, g, mask, Wv, gamma, out):
                     op1=ALU.mult,
                 )
             result = work.tile([P, PACK, N], F32)
-            nc.gpsimd.tensor_tensor(out=result[:], in0=scaled[:], in1=x_rows[:], op=ALU.add)
+            nc.vector.tensor_tensor(out=result[:], in0=scaled[:], in1=x_rows[:], op=ALU.add)
             nc.gpsimd.dma_start(out=out[b].rearrange("(u p) n -> p u n", p=P), in_=result[:])

@@ -48,9 +48,9 @@ def tile_transformer_pa_t_kernel(tc, x, f, g, mask, Wv, gamma, out):
         gamma_col = const.tile([P, 1], F32)
         nc.vector.tensor_copy(out=gamma_col[:], in_=gamma_bf[:])
 
-        mask_rows = const.tile([P, B, N], BF16)
-        for b in range(B):
-            nc.gpsimd.dma_start(out=mask_rows[:, b, :], in_=mask[b].partition_broadcast(P))
+        mask_sb = const.tile([P, N], BF16)
+        nc.vector.memset(mask_sb[:], 0.0)
+        nc.sync.dma_start(out=mask_sb[0:B, :], in_=mask)
 
         w_grouped = const.tile([P, C, PACK], BF16, align_bytes=64)
         for u in range(PACK):
@@ -71,6 +71,17 @@ def tile_transformer_pa_t_kernel(tc, x, f, g, mask, Wv, gamma, out):
             nc.sync.dma_start(out=f_sb[:], in_=f[b])
             g_sb = loads.tile([P, N], BF16)
             nc.sync.dma_start(out=g_sb[:], in_=g[b])
+
+            mask_ps = psum.tile([P, N], F32, tag="s")
+            nc.tensor.matmul(
+                out=mask_ps[:],
+                lhsT=identity[:, b : b + 1].to_broadcast([P, P]),
+                rhs=mask_sb[:],
+                start=True,
+                stop=True,
+            )
+            mask_rows = loads.tile([P, N], BF16)
+            nc.scalar.copy(out=mask_rows[:], in_=mask_ps[:])
 
             x_grouped = work.tile([P, N, PACK], BF16, align_bytes=64)
             nc.scalar.copy(
@@ -152,7 +163,7 @@ def tile_transformer_pa_t_kernel(tc, x, f, g, mask, Wv, gamma, out):
                     out=em_sb[:, v, :],
                     in0=e_sb[:, v, :],
                     scalar=1.0,
-                    in1=mask_rows[:, b, :],
+                    in1=mask_rows[:],
                     op0=ALU.mult,
                     op1=ALU.mult,
                     accum_out=em_sum[:, v : v + 1],
@@ -196,7 +207,7 @@ def tile_transformer_pa_t_kernel(tc, x, f, g, mask, Wv, gamma, out):
                     out=scaled[:, u, :],
                     in0=o_ps[:],
                     scalar=gamma_col[:, 0:1],
-                    in1=mask_rows[:, b, :],
+                    in1=mask_rows[:],
                     op0=ALU.mult,
                     op1=ALU.mult,
                 )

@@ -48,13 +48,17 @@ def tile_transformer_pa_t_kernel(tc, x, f, g, mask, Wv, gamma, out):
         gamma_col = const.tile([P, 1], F32)
         nc.vector.tensor_copy(out=gamma_col[:], in_=gamma_bf[:])
 
+        mask_rows = const.tile([P, B, N], BF16)
+        for b in range(B):
+            nc.gpsimd.dma_start(out=mask_rows[:, b, :], in_=mask[b].partition_broadcast(P))
+
         mask_sb = const.tile([P, N], BF16)
         nc.vector.memset(mask_sb[:], 0.0)
         nc.sync.dma_start(out=mask_sb[0:B, :], in_=mask)
 
         w_grouped = const.tile([P, C, PACK], BF16, align_bytes=64)
         for u in range(PACK):
-            w_t = psum.tile([P, PACK, P], BF16, tag="transposed")
+            w_t = psum.tile([P, PACK, P], BF16, tag="transposed", bufs=1)
             for t in range(PACK):
                 nc.tensor.transpose(w_t[:, t, :], w_rows[:, u, t * P : (t + 1) * P], identity[:])
             nc.vector.tensor_copy(
@@ -72,7 +76,7 @@ def tile_transformer_pa_t_kernel(tc, x, f, g, mask, Wv, gamma, out):
             g_sb = loads.tile([P, N], BF16)
             nc.sync.dma_start(out=g_sb[:], in_=g[b])
 
-            mask_ps = psum.tile([P, N], F32, tag="s")
+            mask_ps = psum.tile([P, N], F32, tag="mask", bufs=1)
             nc.tensor.matmul(
                 out=mask_ps[:],
                 lhsT=identity[:, b : b + 1].to_broadcast([P, P]),
@@ -80,8 +84,6 @@ def tile_transformer_pa_t_kernel(tc, x, f, g, mask, Wv, gamma, out):
                 start=True,
                 stop=True,
             )
-            mask_rows = loads.tile([P, N], BF16)
-            nc.scalar.copy(out=mask_rows[:], in_=mask_ps[:])
 
             x_grouped = work.tile([P, N, PACK], BF16, align_bytes=64)
             nc.scalar.copy(
@@ -114,6 +116,7 @@ def tile_transformer_pa_t_kernel(tc, x, f, g, mask, Wv, gamma, out):
 
             s_sb = work.tile([P, PACK, N], F32)
             s_max = stats.tile([P, PACK], F32)
+            leaky = work.tile([P, PACK, N], F32)
             for v in range(PACK):
                 s_ps = psum.tile([P, N], F32, tag="s")
                 nc.tensor.matmul(
@@ -128,6 +131,14 @@ def tile_transformer_pa_t_kernel(tc, x, f, g, mask, Wv, gamma, out):
                     op1=ALU.max,
                     accum_out=s_max[:, v : v + 1],
                 )
+                nc.vector.scalar_tensor_tensor(
+                    out=leaky[:, v, :],
+                    in0=s_ps[:],
+                    scalar=LEAKY_SLOPE,
+                    in1=s_sb[:, v, :],
+                    op0=ALU.mult,
+                    op1=ALU.max,
+                )
             neg_slope_max = stats.tile([P, PACK], F32)
             nc.vector.tensor_scalar(
                 out=neg_slope_max[:], in0=s_max[:], scalar1=-LEAKY_SLOPE, scalar2=None, op0=ALU.mult
@@ -135,15 +146,6 @@ def tile_transformer_pa_t_kernel(tc, x, f, g, mask, Wv, gamma, out):
             neg_max = stats.tile([P, PACK], F32)
             nc.vector.scalar_tensor_tensor(
                 out=neg_max[:], in0=s_max[:], scalar=-1.0, in1=neg_slope_max[:], op0=ALU.mult, op1=ALU.min
-            )
-            leaky = work.tile([P, PACK, N], F32)
-            nc.vector.scalar_tensor_tensor(
-                out=leaky[:].rearrange("p v i -> p (v i)"),
-                in0=s_sb[:].rearrange("p v i -> p (v i)"),
-                scalar=LEAKY_SLOPE,
-                in1=s_sb[:].rearrange("p v i -> p (v i)"),
-                op0=ALU.mult,
-                op1=ALU.max,
             )
 
             e_sb = work.tile([P, PACK, N], F32)
@@ -163,7 +165,7 @@ def tile_transformer_pa_t_kernel(tc, x, f, g, mask, Wv, gamma, out):
                     out=em_sb[:, v, :],
                     in0=e_sb[:, v, :],
                     scalar=1.0,
-                    in1=mask_rows[:],
+                    in1=mask_ps[:],
                     op0=ALU.mult,
                     op1=ALU.mult,
                     accum_out=em_sum[:, v : v + 1],
@@ -181,7 +183,7 @@ def tile_transformer_pa_t_kernel(tc, x, f, g, mask, Wv, gamma, out):
                 nc.scalar.activation(
                     out=beta_t[:, v, :], in_=em_sb[:, v, :], func=ACT.Copy, scale=recip[:, v : v + 1]
                 )
-                beta_ps = psum.tile([P, PACK, P], BF16, tag="transposed")
+                beta_ps = psum.tile([P, PACK, P], BF16, tag="transposed", bufs=1)
                 for t in range(PACK):
                     nc.tensor.transpose(beta_ps[:, t, :], beta_t[:, v, t * P : (t + 1) * P], identity[:])
                 nc.scalar.copy(
@@ -192,6 +194,7 @@ def tile_transformer_pa_t_kernel(tc, x, f, g, mask, Wv, gamma, out):
             quantise(nc, beta_grouped, beta_codes, beta_scales)
 
             scaled = work.tile([P, PACK, N], F32)
+            result = work.tile([P, PACK, N], F32)
             for u in range(PACK):
                 o_ps = psum.tile([P, N], F32, tag="o")
                 nc.tensor.matmul_mx(
@@ -207,10 +210,11 @@ def tile_transformer_pa_t_kernel(tc, x, f, g, mask, Wv, gamma, out):
                     out=scaled[:, u, :],
                     in0=o_ps[:],
                     scalar=gamma_col[:, 0:1],
-                    in1=mask_rows[:],
+                    in1=mask_rows[:, b, :],
                     op0=ALU.mult,
                     op1=ALU.mult,
                 )
-            result = work.tile([P, PACK, N], F32)
-            nc.vector.tensor_tensor(out=result[:], in0=scaled[:], in1=x_rows[:], op=ALU.add)
+                nc.gpsimd.tensor_tensor(
+                    out=result[:, u, :], in0=scaled[:, u, :], in1=x_rows[:, u, :], op=ALU.add
+                )
             nc.gpsimd.dma_start(out=out[b].rearrange("(u p) n -> p u n", p=P), in_=result[:])

@@ -31,190 +31,254 @@ def quantise(nc, grouped, codes, scales):
 def tile_transformer_pa_t_kernel(tc, x, f, g, mask, Wv, gamma, out):
     nc = tc.nc
     with ExitStack() as stack:
+        stack.enter_context(tc.manual_schedule())
         const = stack.enter_context(tc.tile_pool(name="const", bufs=1))
         loads = stack.enter_context(tc.tile_pool(name="loads", bufs=3))
         work = stack.enter_context(tc.tile_pool(name="work", bufs=2))
-        stats = stack.enter_context(tc.tile_pool(name="stats", bufs=2))
-        psum = stack.enter_context(tc.psum_pool(name="psum", bufs=2))
+        stats = stack.enter_context(tc.tile_pool(name="stats", bufs=3))
+        psum = stack.enter_context(tc.psum_pool(name="psum", bufs=4))
 
-        identity = const.tile([P, P], BF16)
-        make_identity(nc, identity[:])
+        x_rows, f_sb, g_sb = {}, {}, {}
+        x_grouped, x_codes, x_scales = {}, {}, {}
+        h_grouped, h_codes, h_scales = {}, {}, {}
+        s_ps, neg_leaky, neg_top = {}, {}, {}
+        e_sb, e_sum, recip = {}, {}, {}
+        beta_t, beta_ps, beta_grouped, beta_codes, beta_scales = {}, {}, {}, {}, {}
+        o_ps, result = {}, {}
 
-        w_rows = const.tile([P, PACK, C], BF16)
-        nc.sync.dma_start(out=w_rows[:], in_=Wv.rearrange("(u p) c -> p u c", p=P))
+        def load(b):
+            f_sb[b] = loads.tile([P, N], BF16, name="f_sb", tag="f_sb")
+            nc.sync.dma_start(out=f_sb[b][:], in_=f[b])
+            g_sb[b] = loads.tile([P, N], BF16, name="g_sb", tag="g_sb")
+            nc.sync.dma_start(out=g_sb[b][:], in_=g[b])
+            x_rows[b] = loads.tile([P, PACK, N], BF16, name="x_rows", tag="x_rows", bufs=7)
+            nc.sync.dma_start(out=x_rows[b][:], in_=x[b].rearrange("(t p) n -> p t n", p=P))
 
-        gamma_bf = const.tile([P, 1], BF16)
-        nc.sync.dma_start(out=gamma_bf[:], in_=gamma.partition_broadcast(P))
-        gamma_col = const.tile([P, 1], F32)
-        nc.vector.tensor_copy(out=gamma_col[:], in_=gamma_bf[:])
-
-        mask_rows = const.tile([P, B, N], BF16)
-        for b in range(B):
-            nc.gpsimd.dma_start(out=mask_rows[:, b, :], in_=mask[b].partition_broadcast(P))
-
-        mask_sb = const.tile([P, N], BF16)
-        nc.vector.memset(mask_sb[:], 0.0)
-        nc.sync.dma_start(out=mask_sb[0:B, :], in_=mask)
-
-        w_grouped = const.tile([P, C, PACK], BF16, align_bytes=64)
-        for u in range(PACK):
-            w_t = psum.tile([P, PACK, P], BF16, tag="transposed", bufs=1)
-            for t in range(PACK):
-                nc.tensor.transpose(w_t[:, t, :], w_rows[:, u, t * P : (t + 1) * P], identity[:])
-            nc.vector.tensor_copy(
-                out=w_grouped[:, u * P : (u + 1) * P, :], in_=w_t[:].rearrange("p t o -> p o t")
-            )
-        w_codes = const.tile([P, C], U32, align_bytes=64)
-        w_scales = const.tile([P, C], U8, align_bytes=64)
-        quantise(nc, w_grouped, w_codes, w_scales)
-
-        for b in range(B):
-            x_rows = loads.tile([P, PACK, N], BF16, bufs=4)
-            nc.sync.dma_start(out=x_rows[:], in_=x[b].rearrange("(t p) n -> p t n", p=P))
-            f_sb = loads.tile([P, N], BF16)
-            nc.sync.dma_start(out=f_sb[:], in_=f[b])
-            g_sb = loads.tile([P, N], BF16)
-            nc.sync.dma_start(out=g_sb[:], in_=g[b])
-
-            mask_ps = psum.tile([P, N], F32, tag="mask", bufs=1)
-            nc.tensor.matmul(
-                out=mask_ps[:],
-                lhsT=identity[:, b : b + 1].to_broadcast([P, P]),
-                rhs=mask_sb[:],
-                start=True,
-                stop=True,
-            )
-
-            x_grouped = work.tile([P, N, PACK], BF16, align_bytes=64)
+        def regroup_x(b):
+            x_grouped[b] = work.tile([P, N, PACK], BF16, name="x_grouped", tag="x_grouped", align_bytes=64)
             nc.scalar.copy(
-                out=x_grouped[:].rearrange("p (c i) t -> p c t i", i=4),
-                in_=x_rows[:].rearrange("p t (c i) -> p c t i", i=4),
+                out=x_grouped[b][:].rearrange("p (c i) t -> p c t i", i=4),
+                in_=x_rows[b][:].rearrange("p t (c i) -> p c t i", i=4),
             )
-            x_codes = work.tile([P, N], U32, align_bytes=64)
-            x_scales = work.tile([P, N], U8, align_bytes=64)
-            quantise(nc, x_grouped, x_codes, x_scales)
 
-            h_grouped = work.tile([P, C, PACK], BF16, align_bytes=64)
+        def quantise_x(b):
+            x_codes[b] = work.tile([P, N], U32, name="x_codes", tag="x_codes", align_bytes=64)
+            x_scales[b] = work.tile([P, N], U8, name="x_scales", tag="x_scales", align_bytes=64)
+            quantise(nc, x_grouped[b], x_codes[b], x_scales[b])
+
+        def project(b):
+            h_grouped[b] = work.tile([P, C, PACK], BF16, name="h_grouped", tag="h_grouped", align_bytes=64)
             for u in range(PACK):
-                h_ps = psum.tile([P, PACK, P], F32, tag="h")
+                h_ps = psum.tile([P, PACK, P], F32, name="h_ps", tag="h_or_beta")
                 for t in range(PACK):
                     nc.tensor.matmul_mx(
                         out=h_ps[:, t, :],
-                        lhsT=x_codes[:, t * P : (t + 1) * P].bitcast(FP8X4),
-                        lhsT_scale=x_scales[:, t * P : (t + 1) * P],
+                        lhsT=x_codes[b][:, t * P : (t + 1) * P].bitcast(FP8X4),
+                        lhsT_scale=x_scales[b][:, t * P : (t + 1) * P],
                         rhs=w_codes[:, u * P : (u + 1) * P].bitcast(FP8X4),
                         rhs_scale=w_scales[:, u * P : (u + 1) * P],
                         start=True,
                         stop=True,
                     )
                 nc.scalar.copy(
-                    out=h_grouped[:, u * P : (u + 1) * P, :], in_=h_ps[:].rearrange("p t o -> p o t")
+                    out=h_grouped[b][:, u * P : (u + 1) * P, :], in_=h_ps[:].rearrange("p t o -> p o t")
                 )
-            h_codes = work.tile([P, C], U32, align_bytes=64)
-            h_scales = work.tile([P, C], U8, align_bytes=64)
-            quantise(nc, h_grouped, h_codes, h_scales)
 
-            s_sb = work.tile([P, PACK, N], F32)
-            s_max = stats.tile([P, PACK], F32)
-            leaky = work.tile([P, PACK, N], F32)
+        def quantise_h(b):
+            h_codes[b] = work.tile([P, C], U32, name="h_codes", tag="h_codes", bufs=3, align_bytes=64)
+            h_scales[b] = work.tile([P, C], U8, name="h_scales", tag="h_scales", bufs=3, align_bytes=64)
+            quantise(nc, h_grouped[b], h_codes[b], h_scales[b])
+
+        def scores(b, v):
+            s_ps[b, v] = psum.tile([P, N], F32, name="s_ps", tag="s_or_o")
+            nc.tensor.matmul(
+                out=s_ps[b, v][:], lhsT=g_sb[b][:, v * P : (v + 1) * P], rhs=f_sb[b][:], start=True, stop=True
+            )
+
+        def maxima_and_leaky(b):
+            neg_leaky[b] = work.tile([P, PACK, N], F32, name="neg_leaky", tag="neg_leaky")
+            neg_s_max = stats.tile([P, PACK], F32, name="neg_s_max", tag="neg_s_max")
             for v in range(PACK):
-                s_ps = psum.tile([P, N], F32, tag="s")
-                nc.tensor.matmul(
-                    out=s_ps[:], lhsT=g_sb[:, v * P : (v + 1) * P], rhs=f_sb[:], start=True, stop=True
-                )
                 nc.vector.tensor_scalar(
-                    out=s_sb[:, v, :],
-                    in0=s_ps[:],
-                    scalar1=1.0,
+                    out=neg_leaky[b][:, v, :],
+                    in0=s_ps[b, v][:],
+                    scalar1=-1.0,
                     scalar2=None,
                     op0=ALU.mult,
-                    op1=ALU.max,
-                    accum_out=s_max[:, v : v + 1],
+                    op1=ALU.min,
+                    accum_out=neg_s_max[:, v : v + 1],
                 )
+            for v in range(PACK):
                 nc.vector.scalar_tensor_tensor(
-                    out=leaky[:, v, :],
-                    in0=s_ps[:],
-                    scalar=LEAKY_SLOPE,
-                    in1=s_sb[:, v, :],
+                    out=neg_leaky[b][:, v, :],
+                    in0=s_ps[b, v][:],
+                    scalar=-LEAKY_SLOPE,
+                    in1=neg_leaky[b][:, v, :],
                     op0=ALU.mult,
-                    op1=ALU.max,
+                    op1=ALU.min,
                 )
-            neg_slope_max = stats.tile([P, PACK], F32)
-            nc.vector.tensor_scalar(
-                out=neg_slope_max[:], in0=s_max[:], scalar1=-LEAKY_SLOPE, scalar2=None, op0=ALU.mult
-            )
-            neg_max = stats.tile([P, PACK], F32)
+            neg_top[b] = stats.tile([P, PACK], F32, name="neg_top", tag="neg_top")
             nc.vector.scalar_tensor_tensor(
-                out=neg_max[:], in0=s_max[:], scalar=-1.0, in1=neg_slope_max[:], op0=ALU.mult, op1=ALU.min
+                out=neg_top[b][:], in0=neg_s_max[:], scalar=LEAKY_SLOPE, in1=neg_s_max[:], op0=ALU.mult, op1=ALU.min
             )
 
-            e_sb = work.tile([P, PACK, N], F32)
-            e_sum = stats.tile([P, PACK], F32)
-            em_sb = work.tile([P, PACK, N], F32)
-            em_sum = stats.tile([P, PACK], F32)
+        def exponentials(b):
+            e_sb[b] = work.tile([P, PACK, N], F32, name="e_sb", tag="e_sb")
+            e_sum[b] = stats.tile([P, PACK], F32, name="e_sum", tag="e_sum")
             for v in range(PACK):
                 nc.scalar.activation(
-                    out=e_sb[:, v, :],
-                    in_=leaky[:, v, :],
+                    out=e_sb[b][:, v, :],
+                    in_=neg_leaky[b][:, v, :],
                     func=ACT.Exp,
-                    bias=neg_max[:, v : v + 1],
-                    scale=1.0,
-                    accum_out=e_sum[:, v : v + 1],
+                    bias=neg_top[b][:, v : v + 1],
+                    scale=-1.0,
+                    accum_out=e_sum[b][:, v : v + 1],
                 )
+
+        def mask_and_sum(b):
+            em_sum = stats.tile([P, PACK], F32, name="em_sum", tag="em_sum")
+            for v in range(PACK):
                 nc.vector.scalar_tensor_tensor(
-                    out=em_sb[:, v, :],
-                    in0=e_sb[:, v, :],
+                    out=e_sb[b][:, v, :],
+                    in0=e_sb[b][:, v, :],
                     scalar=1.0,
-                    in1=mask_ps[:],
+                    in1=mask_rows[:, b, :],
                     op0=ALU.mult,
                     op1=ALU.mult,
                     accum_out=em_sum[:, v : v + 1],
                 )
-            denom = stats.tile([P, PACK], F32)
+            denom = stats.tile([P, PACK], F32, name="denom", tag="denom")
             nc.vector.scalar_tensor_tensor(
-                out=denom[:], in0=e_sum[:], scalar=EPS, in1=em_sum[:], op0=ALU.mult, op1=ALU.add
+                out=denom[:], in0=e_sum[b][:], scalar=EPS, in1=em_sum[:], op0=ALU.mult, op1=ALU.add
             )
-            recip = stats.tile([P, PACK], F32)
-            nc.vector.reciprocal(out=recip[:], in_=denom[:])
+            recip[b] = stats.tile([P, PACK], F32, name="recip", tag="recip")
+            nc.vector.reciprocal(out=recip[b][:], in_=denom[:])
 
-            beta_t = work.tile([P, PACK, N], BF16)
-            beta_grouped = work.tile([P, N, PACK], BF16, align_bytes=64)
-            for v in range(PACK):
-                nc.scalar.activation(
-                    out=beta_t[:, v, :], in_=em_sb[:, v, :], func=ACT.Copy, scale=recip[:, v : v + 1]
+        def normalise_and_transpose(b, v):
+            if v == 0:
+                beta_t[b] = work.tile([P, PACK, N], BF16, name="beta_t", tag="beta_t")
+            if v % 2 == 0:
+                beta_ps[b, v // 2] = psum.tile([P, 2, PACK, P], BF16, name="beta_ps", tag="h_or_beta")
+            nc.scalar.activation(
+                out=beta_t[b][:, v, :], in_=e_sb[b][:, v, :], func=ACT.Copy, scale=recip[b][:, v : v + 1]
+            )
+            for t in range(PACK):
+                nc.tensor.transpose(
+                    beta_ps[b, v // 2][:, v % 2, t, :], beta_t[b][:, v, t * P : (t + 1) * P], identity[:]
                 )
-                beta_ps = psum.tile([P, PACK, P], BF16, tag="transposed", bufs=1)
-                for t in range(PACK):
-                    nc.tensor.transpose(beta_ps[:, t, :], beta_t[:, v, t * P : (t + 1) * P], identity[:])
+
+        def regroup_beta(b):
+            beta_grouped[b] = work.tile([P, N, PACK], BF16, name="beta_grouped", tag="beta_grouped", align_bytes=64)
+            for w in range(2):
                 nc.scalar.copy(
-                    out=beta_grouped[:, v * P : (v + 1) * P, :], in_=beta_ps[:].rearrange("p t j -> p j t")
+                    out=beta_grouped[b][:, w * 2 * P : (w + 1) * 2 * P, :].rearrange("p (v j) t -> p v j t", v=2),
+                    in_=beta_ps[b, w][:].rearrange("p v t j -> p v j t"),
                 )
-            beta_codes = work.tile([P, N], U32, align_bytes=64)
-            beta_scales = work.tile([P, N], U8, align_bytes=64)
-            quantise(nc, beta_grouped, beta_codes, beta_scales)
 
-            scaled = work.tile([P, PACK, N], F32)
-            result = work.tile([P, PACK, N], F32)
+        def quantise_beta(b):
+            beta_codes[b] = work.tile([P, N], U32, name="beta_codes", tag="beta_codes", align_bytes=64)
+            beta_scales[b] = work.tile([P, N], U8, name="beta_scales", tag="beta_scales", align_bytes=64)
+            quantise(nc, beta_grouped[b], beta_codes[b], beta_scales[b])
+
+        def attend(b):
             for u in range(PACK):
-                o_ps = psum.tile([P, N], F32, tag="o")
+                o_ps[b, u] = psum.tile([P, N], F32, name="o_ps", tag="s_or_o")
                 nc.tensor.matmul_mx(
-                    out=o_ps[:],
-                    lhsT=h_codes[:, u * P : (u + 1) * P].bitcast(FP8X4),
-                    lhsT_scale=h_scales[:, u * P : (u + 1) * P],
-                    rhs=beta_codes[:].bitcast(FP8X4),
-                    rhs_scale=beta_scales[:],
+                    out=o_ps[b, u][:],
+                    lhsT=h_codes[b][:, u * P : (u + 1) * P].bitcast(FP8X4),
+                    lhsT_scale=h_scales[b][:, u * P : (u + 1) * P],
+                    rhs=beta_codes[b][:].bitcast(FP8X4),
+                    rhs_scale=beta_scales[b][:],
                     start=True,
                     stop=True,
                 )
-                nc.vector.scalar_tensor_tensor(
-                    out=scaled[:, u, :],
-                    in0=o_ps[:],
-                    scalar=gamma_col[:, 0:1],
-                    in1=mask_rows[:, b, :],
-                    op0=ALU.mult,
-                    op1=ALU.mult,
-                )
-                nc.gpsimd.tensor_tensor(
-                    out=result[:, u, :], in0=scaled[:, u, :], in1=x_rows[:, u, :], op=ALU.add
-                )
-            nc.gpsimd.dma_start(out=out[b].rearrange("(u p) n -> p u n", p=P), in_=result[:])
+
+        def finish(b, u):
+            if u == 0:
+                result[b] = work.tile([P, PACK, N], F32, name="result", tag="result")
+            nc.vector.scalar_tensor_tensor(
+                out=result[b][:, u, :],
+                in0=o_ps[b, u][:],
+                scalar=gamma_col[:, 0:1],
+                in1=mask_rows[:, b, :],
+                op0=ALU.mult,
+                op1=ALU.mult,
+            )
+            nc.gpsimd.tensor_tensor(
+                out=result[b][:, u, :], in0=result[b][:, u, :], in1=x_rows[b][:, u, :], op=ALU.add
+            )
+
+        def store(b):
+            nc.sync.dma_start(out=out[b].rearrange("(u p) n -> p u n", p=P), in_=result[b][:])
+
+        def on(b):
+            return 0 <= b < B
+
+        load(0)
+        w_rows = const.tile([P, PACK, C], BF16)
+        nc.sync.dma_start(out=w_rows[:], in_=Wv.rearrange("(u p) c -> p u c", p=P))
+        gamma_bf = const.tile([P, 1], BF16)
+        nc.sync.dma_start(out=gamma_bf[:], in_=gamma.partition_broadcast(P))
+        load(1)
+        mask_rows = const.tile([P, B, N], BF16)
+        nc.sync.dma_start(
+            out=mask_rows[:].rearrange("p b n -> p (b n)"), in_=mask.rearrange("b n -> (b n)").partition_broadcast(P)
+        )
+        load(2)
+        identity = const.tile([P, P], BF16)
+        make_identity(nc, identity[:])
+
+        for q in range(PACK):
+            scores(0, q)
+        maxima_and_leaky(0)
+
+        gamma_col = const.tile([P, 1], F32)
+        nc.vector.tensor_copy(out=gamma_col[:], in_=gamma_bf[:])
+
+        w_grouped = const.tile([P, C, PACK], BF16, align_bytes=64)
+        for u in range(PACK):
+            w_t = psum.tile([P, PACK, P], BF16, name="w_t", tag="h_or_beta")
+            for t in range(PACK):
+                nc.tensor.transpose(w_t[:, t, :], w_rows[:, u, t * P : (t + 1) * P], identity[:])
+            nc.scalar.copy(out=w_grouped[:, u * P : (u + 1) * P, :], in_=w_t[:].rearrange("p t o -> p o t"))
+        w_codes = const.tile([P, C], U32, align_bytes=64)
+        w_scales = const.tile([P, C], U8, align_bytes=64)
+        quantise(nc, w_grouped, w_codes, w_scales)
+
+        regroup_x(0)
+        quantise_x(0)
+        regroup_x(1)
+
+        for r in range(B + 3):
+            if on(r + 3):
+                load(r + 3)
+            if on(r - 2):
+                regroup_beta(r - 2)
+            if on(r - 1):
+                mask_and_sum(r - 1)
+            if on(r):
+                project(r)
+            if on(r - 2):
+                quantise_beta(r - 2)
+            if on(r - 3):
+                attend(r - 3)
+            if on(r - 1):
+                quantise_h(r - 1)
+            if on(r + 1):
+                quantise_x(r + 1)
+            if on(r):
+                exponentials(r)
+            for q in range(PACK):
+                if on(r - 3):
+                    finish(r - 3, q)
+                if on(r + 1):
+                    scores(r + 1, q)
+            if on(r - 1):
+                for q in range(PACK):
+                    normalise_and_transpose(r - 1, q)
+            if on(r - 3):
+                store(r - 3)
+            if on(r + 2):
+                regroup_x(r + 2)
+            if on(r + 1):
+                maxima_and_leaky(r + 1)

@@ -16,6 +16,7 @@ P = 128
 PACK = 4
 EPS = 1e-6
 LEAKY_SLOPE = 0.2
+X_COLS_ON_SCALAR = 256
 
 FLOPS = B * (2 * C * C * N + 2 * CQ * N * N + 2 * C * N * N)
 
@@ -42,7 +43,7 @@ def tile_transformer_pa_t_kernel(tc, x, f, g, mask, Wv, gamma, out):
         x_grouped, x_codes, x_scales = {}, {}, {}
         h_grouped, h_codes, h_scales = {}, {}, {}
         s_ps, neg_leaky, neg_top = {}, {}, {}
-        e_sb, e_sum, recip = {}, {}, {}
+        e_sb, e_sum, em_sum, denom, recip = {}, {}, {}, {}, {}
         beta_t, beta_ps, beta_grouped, beta_codes, beta_scales = {}, {}, {}, {}, {}
         o_ps, result = {}, {}
 
@@ -57,8 +58,16 @@ def tile_transformer_pa_t_kernel(tc, x, f, g, mask, Wv, gamma, out):
         def regroup_x(b):
             x_grouped[b] = work.tile([P, N, PACK], BF16, name="x_grouped", tag="x_grouped", align_bytes=64)
             nc.scalar.copy(
-                out=x_grouped[b][:].rearrange("p (c i) t -> p c t i", i=4),
-                in_=x_rows[b][:].rearrange("p t (c i) -> p c t i", i=4),
+                out=x_grouped[b][:, :X_COLS_ON_SCALAR, :].rearrange("p (c i) t -> p c t i", i=4),
+                in_=x_rows[b][:, :, :X_COLS_ON_SCALAR].rearrange("p t (c i) -> p c t i", i=4),
+            )
+            nc.gpsimd.tensor_scalar(
+                out=x_grouped[b][:, X_COLS_ON_SCALAR:, :],
+                in0=x_rows[b][:, :, X_COLS_ON_SCALAR:].rearrange("p t c -> p c t"),
+                scalar1=1.0,
+                scalar2=0.0,
+                op0=ALU.mult,
+                op1=ALU.add,
             )
 
         def quantise_x(b):
@@ -136,7 +145,7 @@ def tile_transformer_pa_t_kernel(tc, x, f, g, mask, Wv, gamma, out):
                 )
 
         def mask_and_sum(b):
-            em_sum = stats.tile([P, PACK], F32, name="em_sum", tag="em_sum")
+            em_sum[b] = stats.tile([P, PACK], F32, name="em_sum", tag="em_sum")
             for v in range(PACK):
                 nc.vector.scalar_tensor_tensor(
                     out=e_sb[b][:, v, :],
@@ -145,14 +154,18 @@ def tile_transformer_pa_t_kernel(tc, x, f, g, mask, Wv, gamma, out):
                     in1=mask_rows[:, b, :],
                     op0=ALU.mult,
                     op1=ALU.mult,
-                    accum_out=em_sum[:, v : v + 1],
+                    accum_out=em_sum[b][:, v : v + 1],
                 )
-            denom = stats.tile([P, PACK], F32, name="denom", tag="denom")
+
+        def denominator(b):
+            denom[b] = stats.tile([P, PACK], F32, name="denom", tag="denom")
             nc.vector.scalar_tensor_tensor(
-                out=denom[:], in0=e_sum[b][:], scalar=EPS, in1=em_sum[:], op0=ALU.mult, op1=ALU.add
+                out=denom[b][:], in0=e_sum[b][:], scalar=EPS, in1=em_sum[b][:], op0=ALU.mult, op1=ALU.add
             )
+
+        def reciprocal(b):
             recip[b] = stats.tile([P, PACK], F32, name="recip", tag="recip")
-            nc.vector.reciprocal(out=recip[b][:], in_=denom[:])
+            nc.vector.reciprocal(out=recip[b][:], in_=denom[b][:])
 
         def normalise_and_transpose(b, v):
             if v == 0:
@@ -260,10 +273,13 @@ def tile_transformer_pa_t_kernel(tc, x, f, g, mask, Wv, gamma, out):
                 project(r)
             if on(r - 2):
                 quantise_beta(r - 2)
+            if on(r - 1):
+                denominator(r - 1)
             if on(r - 3):
                 attend(r - 3)
             if on(r - 1):
                 quantise_h(r - 1)
+                reciprocal(r - 1)
             if on(r + 1):
                 quantise_x(r + 1)
             if on(r):

@@ -220,9 +220,7 @@ def tile_transformer_pa_t_kernel(tc, x, f, g, mask, Wv, gamma, out):
             nc.gpsimd.tensor_tensor(
                 out=result[b][:, u, :], in0=result[b][:, u, :], in1=x_rows[b][:, u, :], op=ALU.add
             )
-
-        def store(b):
-            nc.sync.dma_start(out=out[b].rearrange("(u p) n -> p u n", p=P), in_=result[b][:])
+            nc.sync.dma_start(out=out[b][u * P : (u + 1) * P, :], in_=result[b][:, u, :])
 
         def on(b):
             return 0 <= b < B
@@ -271,17 +269,17 @@ def tile_transformer_pa_t_kernel(tc, x, f, g, mask, Wv, gamma, out):
                 mask_and_sum(r - 1)
             if on(r):
                 project(r)
-            if on(r - 2):
-                quantise_beta(r - 2)
-            if on(r - 1):
-                denominator(r - 1)
             if on(r - 3):
                 attend(r - 3)
             if on(r - 1):
                 quantise_h(r - 1)
-                reciprocal(r - 1)
+                denominator(r - 1)
             if on(r + 1):
                 quantise_x(r + 1)
+            if on(r - 1):
+                reciprocal(r - 1)
+            if on(r - 2):
+                quantise_beta(r - 2)
             if on(r):
                 exponentials(r)
             for q in range(PACK):
@@ -292,8 +290,6 @@ def tile_transformer_pa_t_kernel(tc, x, f, g, mask, Wv, gamma, out):
             if on(r - 1):
                 for q in range(PACK):
                     normalise_and_transpose(r - 1, q)
-            if on(r - 3):
-                store(r - 3)
             if on(r + 2):
                 regroup_x(r + 2)
             if on(r + 1):

@@ -16,7 +16,7 @@ P = 128
 PACK = 4
 EPS = 1e-6
 LEAKY_SLOPE = 0.2
-X_COLS_ON_SCALAR = 256
+X_COLS_ON_SCALAR = 384
 
 FLOPS = B * (2 * C * C * N + 2 * CQ * N * N + 2 * C * N * N)
 

@@ -206,7 +206,7 @@ def tile_transformer_pa_t_kernel(tc, x, f, g, mask, Wv, gamma, out):
                     stop=True,
                 )
 
-        def finish(b, u):
+        def scale_o(b, u):
             if u == 0:
                 result[b] = work.tile([P, PACK, N], F32, name="result", tag="result")
             nc.vector.scalar_tensor_tensor(
@@ -217,10 +217,20 @@ def tile_transformer_pa_t_kernel(tc, x, f, g, mask, Wv, gamma, out):
                 op0=ALU.mult,
                 op1=ALU.mult,
             )
-            nc.gpsimd.tensor_tensor(
+
+        def add_x(engine, b, u):
+            engine.tensor_tensor(
                 out=result[b][:, u, :], in0=result[b][:, u, :], in1=x_rows[b][:, u, :], op=ALU.add
             )
             nc.sync.dma_start(out=out[b][u * P : (u + 1) * P, :], in_=result[b][:, u, :])
+
+        def finish_without_scores(b):
+            scale_o(b, 0)
+            add_x(nc.gpsimd, b, 0)
+            for u in range(1, PACK):
+                scale_o(b, u)
+            for u in range(1, PACK):
+                add_x(nc.vector, b, u)
 
         def on(b):
             return 0 <= b < B
@@ -261,6 +271,7 @@ def tile_transformer_pa_t_kernel(tc, x, f, g, mask, Wv, gamma, out):
         regroup_x(1)
 
         for r in range(B + 3):
+            draining = r > B
             if on(r + 3):
                 load(r + 3)
             if on(r - 2):
@@ -278,15 +289,20 @@ def tile_transformer_pa_t_kernel(tc, x, f, g, mask, Wv, gamma, out):
                 quantise_x(r + 1)
             if on(r - 1):
                 reciprocal(r - 1)
-            if on(r - 2):
+            if on(r - 2) and not draining:
                 quantise_beta(r - 2)
             if on(r):
                 exponentials(r)
+            if on(r - 3) and not on(r + 1):
+                finish_without_scores(r - 3)
             for q in range(PACK):
-                if on(r - 3):
-                    finish(r - 3, q)
+                if on(r - 3) and on(r + 1):
+                    scale_o(r - 3, q)
+                    add_x(nc.gpsimd, r - 3, q)
                 if on(r + 1):
                     scores(r + 1, q)
+            if on(r - 2) and draining:
+                quantise_beta(r - 2)
             if on(r - 1):
                 for q in range(PACK):
                     normalise_and_transpose(r - 1, q)

@@ -17,6 +17,7 @@ PACK = 4
 EPS = 1e-6
 LEAKY_SLOPE = 0.2
 X_COLS_ON_SCALAR = 384
+H, X = 0, 1
 
 FLOPS = B * (2 * C * C * N + 2 * CQ * N * N + 2 * C * N * N)
 
@@ -40,8 +41,7 @@ def tile_transformer_pa_t_kernel(tc, x, f, g, mask, Wv, gamma, out):
         psum = stack.enter_context(tc.psum_pool(name="psum", bufs=4))
 
         x_rows, f_sb, g_sb = {}, {}, {}
-        x_grouped, x_codes, x_scales = {}, {}, {}
-        h_grouped, h_codes, h_scales = {}, {}, {}
+        hx_grouped, hx_codes, hx_scales = {}, {}, {}
         s_ps, neg_leaky, neg_top = {}, {}, {}
         e_sb, e_sum, em_sum, denom, recip = {}, {}, {}, {}, {}
         beta_t, beta_ps, beta_grouped, beta_codes, beta_scales = {}, {}, {}, {}, {}
@@ -52,17 +52,22 @@ def tile_transformer_pa_t_kernel(tc, x, f, g, mask, Wv, gamma, out):
             nc.sync.dma_start(out=f_sb[b][:], in_=f[b])
             g_sb[b] = loads.tile([P, N], BF16, name="g_sb", tag="g_sb")
             nc.sync.dma_start(out=g_sb[b][:], in_=g[b])
-            x_rows[b] = loads.tile([P, PACK, N], BF16, name="x_rows", tag="x_rows", bufs=7)
+            x_rows[b] = loads.tile([P, PACK, N], BF16, name="x_rows", tag="x_rows", bufs=6)
             nc.sync.dma_start(out=x_rows[b][:], in_=x[b].rearrange("(t p) n -> p t n", p=P))
 
+        def grouped(k):
+            if k not in hx_grouped:
+                hx_grouped[k] = work.tile([P, 2, N, PACK], BF16, name="hx_grouped", tag="hx_grouped", align_bytes=64)
+            return hx_grouped[k]
+
         def regroup_x(b):
-            x_grouped[b] = work.tile([P, N, PACK], BF16, name="x_grouped", tag="x_grouped", align_bytes=64)
+            x_grouped = grouped(b - 1)[:, X, :, :]
             nc.scalar.copy(
-                out=x_grouped[b][:, :X_COLS_ON_SCALAR, :].rearrange("p (c i) t -> p c t i", i=4),
+                out=x_grouped[:, :X_COLS_ON_SCALAR, :].rearrange("p (c i) t -> p c t i", i=4),
                 in_=x_rows[b][:, :, :X_COLS_ON_SCALAR].rearrange("p t (c i) -> p c t i", i=4),
             )
             nc.gpsimd.tensor_scalar(
-                out=x_grouped[b][:, X_COLS_ON_SCALAR:, :],
+                out=x_grouped[:, X_COLS_ON_SCALAR:, :],
                 in0=x_rows[b][:, :, X_COLS_ON_SCALAR:].rearrange("p t c -> p c t"),
                 scalar1=1.0,
                 scalar2=0.0,
@@ -70,33 +75,34 @@ def tile_transformer_pa_t_kernel(tc, x, f, g, mask, Wv, gamma, out):
                 op1=ALU.add,
             )
 
-        def quantise_x(b):
-            x_codes[b] = work.tile([P, N], U32, name="x_codes", tag="x_codes", align_bytes=64)
-            x_scales[b] = work.tile([P, N], U8, name="x_scales", tag="x_scales", align_bytes=64)
-            quantise(nc, x_grouped[b], x_codes[b], x_scales[b])
+        def quantise_h_and_x(k):
+            hx_codes[k] = work.tile([P, 2, N], U32, name="hx_codes", tag="hx_codes", align_bytes=64)
+            hx_scales[k] = work.tile([P, 2, N], U8, name="hx_scales", tag="hx_scales", align_bytes=64)
+            first = H if on(k - 1) else X
+            last = X if on(k + 1) else H
+            nc.vector.quantize_mx(
+                out=hx_codes[k][:, first : last + 1, :].rearrange("p s w -> p (s w)").bitcast(FP8X4),
+                scales=hx_scales[k][:, first : last + 1, :].rearrange("p s w -> p (s w)"),
+                in_=grouped(k)[:, first : last + 1, :, :].rearrange("p s w t -> p (s w t)"),
+            )
 
         def project(b):
-            h_grouped[b] = work.tile([P, C, PACK], BF16, name="h_grouped", tag="h_grouped", align_bytes=64)
+            h_grouped = grouped(b + 1)[:, H, :, :]
             for u in range(PACK):
                 h_ps = psum.tile([P, PACK, P], F32, name="h_ps", tag="h_or_beta")
                 for t in range(PACK):
                     nc.tensor.matmul_mx(
                         out=h_ps[:, t, :],
-                        lhsT=x_codes[b][:, t * P : (t + 1) * P].bitcast(FP8X4),
-                        lhsT_scale=x_scales[b][:, t * P : (t + 1) * P],
+                        lhsT=hx_codes[b - 1][:, X, t * P : (t + 1) * P].bitcast(FP8X4),
+                        lhsT_scale=hx_scales[b - 1][:, X, t * P : (t + 1) * P],
                         rhs=w_codes[:, u * P : (u + 1) * P].bitcast(FP8X4),
                         rhs_scale=w_scales[:, u * P : (u + 1) * P],
                         start=True,
                         stop=True,
                     )
                 nc.scalar.copy(
-                    out=h_grouped[b][:, u * P : (u + 1) * P, :], in_=h_ps[:].rearrange("p t o -> p o t")
+                    out=h_grouped[:, u * P : (u + 1) * P, :], in_=h_ps[:].rearrange("p t o -> p o t")
                 )
-
-        def quantise_h(b):
-            h_codes[b] = work.tile([P, C], U32, name="h_codes", tag="h_codes", bufs=3, align_bytes=64)
-            h_scales[b] = work.tile([P, C], U8, name="h_scales", tag="h_scales", bufs=3, align_bytes=64)
-            quantise(nc, h_grouped[b], h_codes[b], h_scales[b])
 
         def scores(b, v):
             s_ps[b, v] = psum.tile([P, N], F32, name="s_ps", tag="s_or_o")
@@ -198,8 +204,8 @@ def tile_transformer_pa_t_kernel(tc, x, f, g, mask, Wv, gamma, out):
                 o_ps[b, u] = psum.tile([P, N], F32, name="o_ps", tag="s_or_o")
                 nc.tensor.matmul_mx(
                     out=o_ps[b, u][:],
-                    lhsT=h_codes[b][:, u * P : (u + 1) * P].bitcast(FP8X4),
-                    lhsT_scale=h_scales[b][:, u * P : (u + 1) * P],
+                    lhsT=hx_codes[b + 1][:, H, u * P : (u + 1) * P].bitcast(FP8X4),
+                    lhsT_scale=hx_scales[b + 1][:, H, u * P : (u + 1) * P],
                     rhs=beta_codes[b][:].bitcast(FP8X4),
                     rhs_scale=beta_scales[b][:],
                     start=True,
@@ -267,46 +273,41 @@ def tile_transformer_pa_t_kernel(tc, x, f, g, mask, Wv, gamma, out):
         quantise(nc, w_grouped, w_codes, w_scales)
 
         regroup_x(0)
-        quantise_x(0)
+        quantise_h_and_x(-1)
         regroup_x(1)
 
-        for r in range(B + 3):
-            draining = r > B
+        for r in range(B + 2):
             if on(r + 3):
                 load(r + 3)
-            if on(r - 2):
-                regroup_beta(r - 2)
             if on(r - 1):
                 mask_and_sum(r - 1)
             if on(r):
                 project(r)
-            if on(r - 3):
-                attend(r - 3)
+            if on(r - 2):
+                quantise_beta(r - 2)
+                attend(r - 2)
             if on(r - 1):
-                quantise_h(r - 1)
                 denominator(r - 1)
-            if on(r + 1):
-                quantise_x(r + 1)
+            if on(r - 1) or on(r + 1):
+                quantise_h_and_x(r)
             if on(r - 1):
                 reciprocal(r - 1)
-            if on(r - 2) and not draining:
-                quantise_beta(r - 2)
             if on(r):
                 exponentials(r)
-            if on(r - 3) and not on(r + 1):
-                finish_without_scores(r - 3)
+            if on(r - 2) and not on(r + 1):
+                finish_without_scores(r - 2)
             for q in range(PACK):
-                if on(r - 3) and on(r + 1):
-                    scale_o(r - 3, q)
-                    add_x(nc.gpsimd, r - 3, q)
+                if on(r - 2) and on(r + 1):
+                    scale_o(r - 2, q)
+                    add_x(nc.gpsimd, r - 2, q)
                 if on(r + 1):
                     scores(r + 1, q)
-            if on(r - 2) and draining:
-                quantise_beta(r - 2)
             if on(r - 1):
                 for q in range(PACK):
                     normalise_and_transpose(r - 1, q)
             if on(r + 2):
                 regroup_x(r + 2)
+            if on(r - 1):
+                regroup_beta(r - 1)
             if on(r + 1):
                 maxima_and_leaky(r + 1)

@@ -262,6 +262,8 @@ def tile_transformer_pa_t_kernel(tc, x, f, g, mask, Wv, gamma, out):
         gamma_col = const.tile([P, 1], F32)
         nc.vector.tensor_copy(out=gamma_col[:], in_=gamma_bf[:])
 
+        regroup_x(0)
+
         w_grouped = const.tile([P, C, PACK], BF16, align_bytes=64)
         for u in range(PACK):
             w_t = psum.tile([P, PACK, P], BF16, name="w_t", tag="h_or_beta")
@@ -272,7 +274,6 @@ def tile_transformer_pa_t_kernel(tc, x, f, g, mask, Wv, gamma, out):
         w_scales = const.tile([P, C], U8, align_bytes=64)
         quantise(nc, w_grouped, w_codes, w_scales)
 
-        regroup_x(0)
         quantise_h_and_x(-1)
         regroup_x(1)
 

@@ -45,7 +45,7 @@ def tile_transformer_pa_t_kernel(tc, x, f, g, mask, Wv, gamma, out):
         s_ps, neg_leaky, neg_top = {}, {}, {}
         e_sb, e_sum, em_sum, denom, recip = {}, {}, {}, {}, {}
         beta_t, beta_ps, beta_grouped, beta_codes, beta_scales = {}, {}, {}, {}, {}
-        o_ps, result = {}, {}
+        o_ps, scaled, result = {}, {}, {}
 
         def load(b):
             f_sb[b] = loads.tile([P, N], BF16, name="f_sb", tag="f_sb")
@@ -214,9 +214,9 @@ def tile_transformer_pa_t_kernel(tc, x, f, g, mask, Wv, gamma, out):
 
         def scale_o(b, u):
             if u == 0:
-                result[b] = work.tile([P, PACK, N], F32, name="result", tag="result")
+                scaled[b] = work.tile([P, PACK, N], F32, name="scaled", tag="scaled")
             nc.vector.scalar_tensor_tensor(
-                out=result[b][:, u, :],
+                out=scaled[b][:, u, :],
                 in0=o_ps[b, u][:],
                 scalar=gamma_col[:, 0:1],
                 in1=mask_rows[:, b, :],
@@ -225,8 +225,10 @@ def tile_transformer_pa_t_kernel(tc, x, f, g, mask, Wv, gamma, out):
             )
 
         def add_x(engine, b, u):
+            if u == 0:
+                result[b] = work.tile([P, PACK, N], F32, name="result", tag="result")
             engine.tensor_tensor(
-                out=result[b][:, u, :], in0=result[b][:, u, :], in1=x_rows[b][:, u, :], op=ALU.add
+                out=result[b][:, u, :], in0=scaled[b][:, u, :], in1=x_rows[b][:, u, :], op=ALU.add
             )
             nc.sync.dma_start(out=out[b][u * P : (u + 1) * P, :], in_=result[b][:, u, :])
 

@@ -16,7 +16,7 @@ P = 128
 PACK = 4
 EPS = 1e-6
 LEAKY_SLOPE = 0.2
-X_COLS_ON_SCALAR = 384
+X_COLS_ON_SCALAR = 448
 H, X = 0, 1
 
 FLOPS = B * (2 * C * C * N + 2 * CQ * N * N + 2 * C * N * N)

@@ -16,7 +16,7 @@ P = 128
 PACK = 4
 EPS = 1e-6
 LEAKY_SLOPE = 0.2
-X_COLS_ON_SCALAR = 448
+X_COLS_ON_SCALAR_AT_START = 256
 H, X = 0, 1
 
 FLOPS = B * (2 * C * C * N + 2 * CQ * N * N + 2 * C * N * N)
@@ -42,10 +42,10 @@ def tile_transformer_pa_t_kernel(tc, x, f, g, mask, Wv, gamma, out):
 
         x_rows, f_sb, g_sb = {}, {}, {}
         hx_grouped, hx_codes, hx_scales = {}, {}, {}
-        s_ps, neg_leaky, neg_top = {}, {}, {}
+        h_ps, s_ps, neg_leaky, neg_s_max, neg_top = {}, {}, {}, {}, {}
         e_sb, e_sum, em_sum, denom, recip = {}, {}, {}, {}, {}
         beta_t, beta_ps, beta_grouped, beta_codes, beta_scales = {}, {}, {}, {}, {}
-        o_ps, scaled, result = {}, {}, {}
+        o_ps, ot_ps, scaled, scaled_t, sum_ps, result = {}, {}, {}, {}, {}, {}
 
         def load(b):
             f_sb[b] = loads.tile([P, N], BF16, name="f_sb", tag="f_sb")
@@ -60,15 +60,16 @@ def tile_transformer_pa_t_kernel(tc, x, f, g, mask, Wv, gamma, out):
                 hx_grouped[k] = work.tile([P, 2, N, PACK], BF16, name="hx_grouped", tag="hx_grouped", align_bytes=64)
             return hx_grouped[k]
 
-        def regroup_x(b):
-            x_grouped = grouped(b - 1)[:, X, :, :]
+        def regroup_x_on_scalar(b, first, last):
             nc.scalar.copy(
-                out=x_grouped[:, :X_COLS_ON_SCALAR, :].rearrange("p (c i) t -> p c t i", i=4),
-                in_=x_rows[b][:, :, :X_COLS_ON_SCALAR].rearrange("p t (c i) -> p c t i", i=4),
+                out=grouped(b - 1)[:, X, first:last, :].rearrange("p (c i) t -> p c t i", i=4),
+                in_=x_rows[b][:, :, first:last].rearrange("p t (c i) -> p c t i", i=4),
             )
+
+        def regroup_x_on_gpsimd(b, first, last):
             nc.gpsimd.tensor_scalar(
-                out=x_grouped[:, X_COLS_ON_SCALAR:, :],
-                in0=x_rows[b][:, :, X_COLS_ON_SCALAR:].rearrange("p t c -> p c t"),
+                out=grouped(b - 1)[:, X, first:last, :],
+                in0=x_rows[b][:, :, first:last].rearrange("p t c -> p c t"),
                 scalar1=1.0,
                 scalar2=0.0,
                 op0=ALU.mult,
@@ -86,23 +87,23 @@ def tile_transformer_pa_t_kernel(tc, x, f, g, mask, Wv, gamma, out):
                 in_=grouped(k)[:, first : last + 1, :, :].rearrange("p s w t -> p (s w t)"),
             )
 
-        def project(b):
-            h_grouped = grouped(b + 1)[:, H, :, :]
-            for u in range(PACK):
-                h_ps = psum.tile([P, PACK, P], F32, name="h_ps", tag="h_or_beta")
-                for t in range(PACK):
-                    nc.tensor.matmul_mx(
-                        out=h_ps[:, t, :],
-                        lhsT=hx_codes[b - 1][:, X, t * P : (t + 1) * P].bitcast(FP8X4),
-                        lhsT_scale=hx_scales[b - 1][:, X, t * P : (t + 1) * P],
-                        rhs=w_codes[:, u * P : (u + 1) * P].bitcast(FP8X4),
-                        rhs_scale=w_scales[:, u * P : (u + 1) * P],
-                        start=True,
-                        stop=True,
-                    )
-                nc.scalar.copy(
-                    out=h_grouped[:, u * P : (u + 1) * P, :], in_=h_ps[:].rearrange("p t o -> p o t")
+        def project(b, u):
+            h_ps[b, u] = psum.tile([P, PACK, P], F32, name="h_ps", tag="h_or_beta")
+            for t in range(PACK):
+                nc.tensor.matmul_mx(
+                    out=h_ps[b, u][:, t, :],
+                    lhsT=hx_codes[b - 1][:, X, t * P : (t + 1) * P].bitcast(FP8X4),
+                    lhsT_scale=hx_scales[b - 1][:, X, t * P : (t + 1) * P],
+                    rhs=w_codes[:, u * P : (u + 1) * P].bitcast(FP8X4),
+                    rhs_scale=w_scales[:, u * P : (u + 1) * P],
+                    start=True,
+                    stop=True,
                 )
+
+        def copy_h(b, u):
+            nc.scalar.copy(
+                out=grouped(b + 1)[:, H, u * P : (u + 1) * P, :], in_=h_ps[b, u][:].rearrange("p t o -> p o t")
+            )
 
         def scores(b, v):
             s_ps[b, v] = psum.tile([P, N], F32, name="s_ps", tag="s_or_o")
@@ -110,58 +111,66 @@ def tile_transformer_pa_t_kernel(tc, x, f, g, mask, Wv, gamma, out):
                 out=s_ps[b, v][:], lhsT=g_sb[b][:, v * P : (v + 1) * P], rhs=f_sb[b][:], start=True, stop=True
             )
 
-        def maxima_and_leaky(b):
-            neg_leaky[b] = work.tile([P, PACK, N], F32, name="neg_leaky", tag="neg_leaky")
-            neg_s_max = stats.tile([P, PACK], F32, name="neg_s_max", tag="neg_s_max")
-            for v in range(PACK):
-                nc.vector.tensor_scalar(
-                    out=neg_leaky[b][:, v, :],
-                    in0=s_ps[b, v][:],
-                    scalar1=-1.0,
-                    scalar2=None,
-                    op0=ALU.mult,
-                    op1=ALU.min,
-                    accum_out=neg_s_max[:, v : v + 1],
-                )
-            for v in range(PACK):
-                nc.vector.scalar_tensor_tensor(
-                    out=neg_leaky[b][:, v, :],
-                    in0=s_ps[b, v][:],
-                    scalar=-LEAKY_SLOPE,
-                    in1=neg_leaky[b][:, v, :],
-                    op0=ALU.mult,
-                    op1=ALU.min,
-                )
-            neg_top[b] = stats.tile([P, PACK], F32, name="neg_top", tag="neg_top")
-            nc.vector.scalar_tensor_tensor(
-                out=neg_top[b][:], in0=neg_s_max[:], scalar=LEAKY_SLOPE, in1=neg_s_max[:], op0=ALU.mult, op1=ALU.min
+        def maximum(b, v):
+            if v == 0:
+                neg_leaky[b] = work.tile([P, PACK, N], F32, name="neg_leaky", tag="neg_leaky")
+                neg_s_max[b] = stats.tile([P, PACK], F32, name="neg_s_max", tag="neg_s_max")
+            nc.vector.tensor_scalar(
+                out=neg_leaky[b][:, v, :],
+                in0=s_ps[b, v][:],
+                scalar1=-1.0,
+                scalar2=None,
+                op0=ALU.mult,
+                op1=ALU.min,
+                accum_out=neg_s_max[b][:, v : v + 1],
             )
 
-        def exponentials(b):
-            e_sb[b] = work.tile([P, PACK, N], F32, name="e_sb", tag="e_sb")
-            e_sum[b] = stats.tile([P, PACK], F32, name="e_sum", tag="e_sum")
-            for v in range(PACK):
-                nc.scalar.activation(
-                    out=e_sb[b][:, v, :],
-                    in_=neg_leaky[b][:, v, :],
-                    func=ACT.Exp,
-                    bias=neg_top[b][:, v : v + 1],
-                    scale=-1.0,
-                    accum_out=e_sum[b][:, v : v + 1],
-                )
+        def leaky(b, v):
+            nc.vector.scalar_tensor_tensor(
+                out=neg_leaky[b][:, v, :],
+                in0=s_ps[b, v][:],
+                scalar=-LEAKY_SLOPE,
+                in1=neg_leaky[b][:, v, :],
+                op0=ALU.mult,
+                op1=ALU.min,
+            )
 
-        def mask_and_sum(b):
-            em_sum[b] = stats.tile([P, PACK], F32, name="em_sum", tag="em_sum")
-            for v in range(PACK):
-                nc.vector.scalar_tensor_tensor(
-                    out=e_sb[b][:, v, :],
-                    in0=e_sb[b][:, v, :],
-                    scalar=1.0,
-                    in1=mask_rows[:, b, :],
-                    op0=ALU.mult,
-                    op1=ALU.mult,
-                    accum_out=em_sum[b][:, v : v + 1],
-                )
+        def top(b):
+            neg_top[b] = stats.tile([P, PACK], F32, name="neg_top", tag="neg_top")
+            nc.vector.scalar_tensor_tensor(
+                out=neg_top[b][:],
+                in0=neg_s_max[b][:],
+                scalar=LEAKY_SLOPE,
+                in1=neg_s_max[b][:],
+                op0=ALU.mult,
+                op1=ALU.min,
+            )
+
+        def exponential(b, v):
+            if v == 0:
+                e_sb[b] = work.tile([P, PACK, N], F32, name="e_sb", tag="e_sb")
+                e_sum[b] = stats.tile([P, PACK], F32, name="e_sum", tag="e_sum")
+            nc.scalar.activation(
+                out=e_sb[b][:, v, :],
+                in_=neg_leaky[b][:, v, :],
+                func=ACT.Exp,
+                bias=neg_top[b][:, v : v + 1],
+                scale=-1.0,
+                accum_out=e_sum[b][:, v : v + 1],
+            )
+
+        def mask_and_sum(b, v):
+            if v == 0:
+                em_sum[b] = stats.tile([P, PACK], F32, name="em_sum", tag="em_sum")
+            nc.vector.scalar_tensor_tensor(
+                out=e_sb[b][:, v, :],
+                in0=e_sb[b][:, v, :],
+                scalar=1.0,
+                in1=mask_rows[:, b, :],
+                op0=ALU.mult,
+                op1=ALU.mult,
+                accum_out=em_sum[b][:, v : v + 1],
+            )
 
         def denominator(b):
             denom[b] = stats.tile([P, PACK], F32, name="denom", tag="denom")
@@ -183,16 +192,18 @@ def tile_transformer_pa_t_kernel(tc, x, f, g, mask, Wv, gamma, out):
             )
             for t in range(PACK):
                 nc.tensor.transpose(
-                    beta_ps[b, v // 2][:, v % 2, t, :], beta_t[b][:, v, t * P : (t + 1) * P], identity[:]
+                    beta_ps[b, v // 2][:, v % 2, t, :], beta_t[b][:, v, t * P : (t + 1) * P], identity_bf[:]
                 )
 
-        def regroup_beta(b):
-            beta_grouped[b] = work.tile([P, N, PACK], BF16, name="beta_grouped", tag="beta_grouped", align_bytes=64)
-            for w in range(2):
-                nc.scalar.copy(
-                    out=beta_grouped[b][:, w * 2 * P : (w + 1) * 2 * P, :].rearrange("p (v j) t -> p v j t", v=2),
-                    in_=beta_ps[b, w][:].rearrange("p v t j -> p v j t"),
+        def regroup_beta(b, w):
+            if w == 0:
+                beta_grouped[b] = work.tile(
+                    [P, N, PACK], BF16, name="beta_grouped", tag="beta_grouped", align_bytes=64
                 )
+            nc.scalar.copy(
+                out=beta_grouped[b][:, w * 2 * P : (w + 1) * 2 * P, :].rearrange("p (v j) t -> p v j t", v=2),
+                in_=beta_ps[b, w][:].rearrange("p v t j -> p v j t"),
+            )
 
         def quantise_beta(b):
             beta_codes[b] = work.tile([P, N], U32, name="beta_codes", tag="beta_codes", align_bytes=64)
@@ -200,7 +211,19 @@ def tile_transformer_pa_t_kernel(tc, x, f, g, mask, Wv, gamma, out):
             quantise(nc, beta_grouped[b], beta_codes[b], beta_scales[b])
 
         def attend(b):
-            for u in range(PACK):
+            for v in range(PACK):
+                if v % 2 == 0:
+                    ot_ps[b, v // 2] = psum.tile([P, 2, 2 * P], F32, name="ot_ps", tag="s_or_o")
+                nc.tensor.matmul_mx(
+                    out=ot_ps[b, v // 2][:, v % 2, :],
+                    lhsT=beta_codes[b][:, v * P : (v + 1) * P].bitcast(FP8X4),
+                    lhsT_scale=beta_scales[b][:, v * P : (v + 1) * P],
+                    rhs=hx_codes[b + 1][:, H, 2 * P :].bitcast(FP8X4),
+                    rhs_scale=hx_scales[b + 1][:, H, 2 * P :],
+                    start=True,
+                    stop=True,
+                )
+            for u in range(2):
                 o_ps[b, u] = psum.tile([P, N], F32, name="o_ps", tag="s_or_o")
                 nc.tensor.matmul_mx(
                     out=o_ps[b, u][:],
@@ -214,7 +237,7 @@ def tile_transformer_pa_t_kernel(tc, x, f, g, mask, Wv, gamma, out):
 
         def scale_o(b, u):
             if u == 0:
-                scaled[b] = work.tile([P, PACK, N], F32, name="scaled", tag="scaled")
+                scaled[b] = work.tile([P, 2, N], F32, name="scaled", tag="scaled")
             nc.vector.scalar_tensor_tensor(
                 out=scaled[b][:, u, :],
                 in0=o_ps[b, u][:],
@@ -224,21 +247,43 @@ def tile_transformer_pa_t_kernel(tc, x, f, g, mask, Wv, gamma, out):
                 op1=ALU.mult,
             )
 
+        def scale_ot(b, v):
+            if v == 0:
+                scaled_t[b] = work.tile([P, PACK, 2 * P], F32, name="scaled_t", tag="scaled_t")
+            nc.scalar.activation(
+                out=scaled_t[b][:, v, :],
+                in_=ot_ps[b, v // 2][:, v % 2, :],
+                func=ACT.Copy,
+                scale=gamma_mask_cols[:, PACK * b + v : PACK * b + v + 1],
+            )
+
+        def store(b, u):
+            nc.sync.dma_start(out=out[b][u * P : (u + 1) * P, :], in_=result[b][:, u, :])
+
         def add_x(engine, b, u):
             if u == 0:
                 result[b] = work.tile([P, PACK, N], F32, name="result", tag="result")
             engine.tensor_tensor(
                 out=result[b][:, u, :], in0=scaled[b][:, u, :], in1=x_rows[b][:, u, :], op=ALU.add
             )
-            nc.sync.dma_start(out=out[b][u * P : (u + 1) * P, :], in_=result[b][:, u, :])
+            store(b, u)
 
-        def finish_without_scores(b):
-            scale_o(b, 0)
-            add_x(nc.gpsimd, b, 0)
-            for u in range(1, PACK):
-                scale_o(b, u)
-            for u in range(1, PACK):
-                add_x(nc.vector, b, u)
+        def add_x_in_psum(b, u):
+            sum_ps[b, u] = psum.tile([P, N], F32, name="sum_ps", tag="h_or_beta")
+            nc.tensor.matmul(out=sum_ps[b, u][:], lhsT=identity_bf[:], rhs=x_rows[b][:, u, :], start=True, stop=False)
+            for v in range(PACK):
+                nc.tensor.matmul(
+                    out=sum_ps[b, u][:, v * P : (v + 1) * P],
+                    lhsT=scaled_t[b][:, v, (u - 2) * P : (u - 1) * P],
+                    rhs=identity[:],
+                    is_transpose=True,
+                    start=False,
+                    stop=v == PACK - 1,
+                )
+
+        def copy_sum(b, u):
+            nc.scalar.copy(out=result[b][:, u, :], in_=sum_ps[b, u][:])
+            store(b, u)
 
         def on(b):
             return 0 <= b < B
@@ -248,69 +293,186 @@ def tile_transformer_pa_t_kernel(tc, x, f, g, mask, Wv, gamma, out):
         nc.sync.dma_start(out=w_rows[:], in_=Wv.rearrange("(u p) c -> p u c", p=P))
         gamma_bf = const.tile([P, 1], BF16)
         nc.sync.dma_start(out=gamma_bf[:], in_=gamma.partition_broadcast(P))
+        mask_tiles = const.tile([P, P], BF16)
+        for half in range(2):
+            nc.sync.dma_start(
+                out=mask_tiles[half * B * PACK : (half + 1) * B * PACK, :],
+                in_=mask.rearrange("b (t p) -> (b t) p", p=P),
+            )
         load(1)
         mask_rows = const.tile([P, B, N], BF16)
         nc.sync.dma_start(
             out=mask_rows[:].rearrange("p b n -> p (b n)"), in_=mask.rearrange("b n -> (b n)").partition_broadcast(P)
         )
         load(2)
-        identity = const.tile([P, P], BF16)
+        identity_bf = const.tile([P, P], BF16)
+        make_identity(nc, identity_bf[:])
+        identity = const.tile([P, P], F32)
         make_identity(nc, identity[:])
 
         for q in range(PACK):
             scores(0, q)
-        maxima_and_leaky(0)
+        for v in range(PACK):
+            maximum(0, v)
+        for v in range(PACK):
+            leaky(0, v)
+        top(0)
 
         gamma_col = const.tile([P, 1], F32)
         nc.vector.tensor_copy(out=gamma_col[:], in_=gamma_bf[:])
 
-        regroup_x(0)
+        regroup_x_on_scalar(0, 0, 256)
+        regroup_x_on_gpsimd(0, 256, N)
 
         w_grouped = const.tile([P, C, PACK], BF16, align_bytes=64)
         for u in range(PACK):
             w_t = psum.tile([P, PACK, P], BF16, name="w_t", tag="h_or_beta")
             for t in range(PACK):
-                nc.tensor.transpose(w_t[:, t, :], w_rows[:, u, t * P : (t + 1) * P], identity[:])
+                nc.tensor.transpose(w_t[:, t, :], w_rows[:, u, t * P : (t + 1) * P], identity_bf[:])
             nc.scalar.copy(out=w_grouped[:, u * P : (u + 1) * P, :], in_=w_t[:].rearrange("p t o -> p o t"))
         w_codes = const.tile([P, C], U32, align_bytes=64)
         w_scales = const.tile([P, C], U8, align_bytes=64)
         quantise(nc, w_grouped, w_codes, w_scales)
-
         quantise_h_and_x(-1)
-        regroup_x(1)
 
-        for r in range(B + 2):
+        mask_t = psum.tile([P, P], BF16, name="mask_t", tag="h_or_beta")
+        nc.tensor.transpose(mask_t[:], mask_tiles[:], identity_bf[:])
+        gamma_mask_cols = const.tile([P, B * PACK], F32)
+        nc.vector.tensor_scalar(
+            out=gamma_mask_cols[:], in0=mask_t[:, : B * PACK], scalar1=gamma_col[:, 0:1], scalar2=None, op0=ALU.mult
+        )
+        for q in range(PACK):
+            scores(1, q)
+        regroup_x_on_scalar(1, 0, 256)
+        regroup_x_on_gpsimd(1, 256, N)
+
+        for r in range(B - 1):
             if on(r + 3):
                 load(r + 3)
+            for u in range(PACK):
+                project(r, u)
+            if r == 0:
+                for v in range(PACK):
+                    exponential(r, v)
+            for u in range(PACK):
+                copy_h(r, u)
             if on(r - 1):
-                mask_and_sum(r - 1)
-            if on(r):
-                project(r)
+                mask_and_sum(r - 1, 0)
+                mask_and_sum(r - 1, 1)
             if on(r - 2):
                 quantise_beta(r - 2)
                 attend(r - 2)
             if on(r - 1):
+                mask_and_sum(r - 1, 2)
+                mask_and_sum(r - 1, 3)
+            quantise_h_and_x(r)
+            if on(r - 1):
                 denominator(r - 1)
-            if on(r - 1) or on(r + 1):
-                quantise_h_and_x(r)
+            if r > 0:
+                exponential(r, 0)
+            if on(r - 2):
+                for v in range(PACK):
+                    scale_ot(r - 2, v)
+                    if v % 2 == 1:
+                        scores(r + 1, v // 2)
+                scale_o(r - 2, 0)
             if on(r - 1):
                 reciprocal(r - 1)
-            if on(r):
-                exponentials(r)
-            if on(r - 2) and not on(r + 1):
-                finish_without_scores(r - 2)
-            for q in range(PACK):
-                if on(r - 2) and on(r + 1):
-                    scale_o(r - 2, q)
-                    add_x(nc.gpsimd, r - 2, q)
-                if on(r + 1):
+            if on(r - 2):
+                scores(r + 1, 2)
+                scale_o(r - 2, 1)
+                scores(r + 1, 3)
+                add_x(nc.gpsimd, r - 2, 0)
+                add_x(nc.gpsimd, r - 2, 1)
+            elif r == 1:
+                for q in range(PACK):
                     scores(r + 1, q)
+            if r > 0:
+                for v in range(1, PACK):
+                    exponential(r, v)
+            if on(r - 2):
+                add_x_in_psum(r - 2, 2)
+                add_x_in_psum(r - 2, 3)
             if on(r - 1):
                 for q in range(PACK):
                     normalise_and_transpose(r - 1, q)
+            if on(r - 2):
+                copy_sum(r - 2, 2)
+                copy_sum(r - 2, 3)
             if on(r + 2):
-                regroup_x(r + 2)
+                for first in range(0, N, 256):
+                    regroup_x_on_gpsimd(r + 2, first, first + 256)
             if on(r - 1):
-                regroup_beta(r - 1)
-            if on(r + 1):
-                maxima_and_leaky(r + 1)
+                for w in range(2):
+                    regroup_beta(r - 1, w)
+            for v in range(PACK):
+                maximum(r + 1, v)
+            for v in range(PACK):
+                leaky(r + 1, v)
+            top(r + 1)
+
+        w, z, y = B - 3, B - 2, B - 1
+        for u in range(PACK):
+            project(y, u)
+        mask_and_sum(z, 0)
+        mask_and_sum(z, 1)
+        quantise_beta(w)
+        attend(w)
+        mask_and_sum(z, 2)
+        mask_and_sum(z, 3)
+        quantise_h_and_x(y)
+        denominator(z)
+        for v in range(PACK):
+            exponential(y, v)
+        for v in range(PACK):
+            scale_ot(w, v)
+        scale_o(w, 0)
+        reciprocal(z)
+        scale_o(w, 1)
+        add_x(nc.gpsimd, w, 0)
+        add_x(nc.vector, w, 1)
+        copy_h(y, 0)
+        copy_h(y, 1)
+        for q in range(PACK):
+            normalise_and_transpose(z, q)
+        copy_h(y, 2)
+        copy_h(y, 3)
+        for v in range(2):
+            regroup_beta(z, v)
+        for u in range(2, PACK):
+            add_x_in_psum(w, u)
+        for u in range(2, PACK):
+            copy_sum(w, u)
+        for v in range(PACK):
+            mask_and_sum(y, v)
+        denominator(y)
+        quantise_beta(z)
+        attend(z)
+        reciprocal(y)
+        quantise_h_and_x(B)
+        for q in range(PACK):
+            normalise_and_transpose(y, q)
+        for v in range(PACK):
+            scale_ot(z, v)
+        for v in range(2):
+            regroup_beta(y, v)
+        scale_o(z, 0)
+        scale_o(z, 1)
+        add_x(nc.gpsimd, z, 0)
+        add_x(nc.vector, z, 1)
+        for u in range(2, PACK):
+            add_x_in_psum(z, u)
+        for u in range(2, PACK):
+            copy_sum(z, u)
+        quantise_beta(y)
+        attend(y)
+        for v in range(PACK):
+            scale_ot(y, v)
+        scale_o(y, 0)
+        scale_o(y, 1)
+        add_x(nc.gpsimd, y, 0)
+        add_x(nc.vector, y, 1)
+        for u in range(2, PACK):
+            add_x_in_psum(y, u)
+        for u in range(2, PACK):
+            copy_sum(y, u)

@@ -17,6 +17,7 @@ PACK = 4
 EPS = 1e-6
 LEAKY_SLOPE = 0.2
 X_COLS_ON_SCALAR_AT_START = 256
+SCALAR, GPSIMD = 0, 1
 H, X = 0, 1
 
 FLOPS = B * (2 * C * C * N + 2 * CQ * N * N + 2 * C * N * N)
@@ -60,21 +61,15 @@ def tile_transformer_pa_t_kernel(tc, x, f, g, mask, Wv, gamma, out):
                 hx_grouped[k] = work.tile([P, 2, N, PACK], BF16, name="hx_grouped", tag="hx_grouped", align_bytes=64)
             return hx_grouped[k]
 
-        def regroup_x_on_scalar(b, first, last):
-            nc.scalar.copy(
-                out=grouped(b - 1)[:, X, first:last, :].rearrange("p (c i) t -> p c t i", i=4),
-                in_=x_rows[b][:, :, first:last].rearrange("p t (c i) -> p c t i", i=4),
-            )
-
-        def regroup_x_on_gpsimd(b, first, last):
-            nc.gpsimd.tensor_scalar(
-                out=grouped(b - 1)[:, X, first:last, :],
-                in0=x_rows[b][:, :, first:last].rearrange("p t c -> p c t"),
-                scalar1=1.0,
-                scalar2=0.0,
-                op0=ALU.mult,
-                op1=ALU.add,
-            )
+        def regroup_x(engine, b, u):
+            source = x_rows[b][:, :, u * 2 * P : (u + 1) * 2 * P].rearrange("p t (q e) -> p e q t", e=2)
+            target = grouped(b - 1)[:, X, u * 2 * P : (u + 1) * 2 * P, :].rearrange("p (e q) t -> p e q t", e=2)
+            if engine == SCALAR:
+                nc.scalar.copy(out=target, in_=source)
+            else:
+                nc.gpsimd.tensor_scalar(
+                    out=target, in0=source, scalar1=1.0, scalar2=0.0, op0=ALU.mult, op1=ALU.add
+                )
 
         def quantise_h_and_x(k):
             hx_codes[k] = work.tile([P, 2, N], U32, name="hx_codes", tag="hx_codes", align_bytes=64)
@@ -186,23 +181,23 @@ def tile_transformer_pa_t_kernel(tc, x, f, g, mask, Wv, gamma, out):
             if v == 0:
                 beta_t[b] = work.tile([P, PACK, N], BF16, name="beta_t", tag="beta_t")
             if v % 2 == 0:
-                beta_ps[b, v // 2] = psum.tile([P, 2, PACK, P], BF16, name="beta_ps", tag="h_or_beta")
+                beta_ps[b, v // 2] = psum.tile([P, 2, 2, P], F32, name="beta_ps", tag="h_or_beta")
             nc.scalar.activation(
                 out=beta_t[b][:, v, :], in_=e_sb[b][:, v, :], func=ACT.Copy, scale=recip[b][:, v : v + 1]
             )
-            for t in range(PACK):
-                nc.tensor.transpose(
-                    beta_ps[b, v // 2][:, v % 2, t, :], beta_t[b][:, v, t * P : (t + 1) * P], identity_bf[:]
-                )
+            words = beta_t[b][:, v, :].bitcast(F32)
+            for u in range(2):
+                nc.tensor.transpose(beta_ps[b, v // 2][:, v % 2, u, :], words[:, u * P : (u + 1) * P], identity[:])
 
         def regroup_beta(b, w):
             if w == 0:
                 beta_grouped[b] = work.tile(
                     [P, N, PACK], BF16, name="beta_grouped", tag="beta_grouped", align_bytes=64
                 )
+            words = beta_grouped[b][:, w * 2 * P : (w + 1) * 2 * P, :].rearrange("p n t -> p (n t)").bitcast(F32)
             nc.scalar.copy(
-                out=beta_grouped[b][:, w * 2 * P : (w + 1) * 2 * P, :].rearrange("p (v j) t -> p v j t", v=2),
-                in_=beta_ps[b, w][:].rearrange("p v t j -> p v j t"),
+                out=words.rearrange("p (v j u) -> p v j u", v=2, u=2),
+                in_=beta_ps[b, w][:].rearrange("p v u j -> p v j u"),
             )
 
         def quantise_beta(b):
@@ -321,8 +316,8 @@ def tile_transformer_pa_t_kernel(tc, x, f, g, mask, Wv, gamma, out):
         gamma_col = const.tile([P, 1], F32)
         nc.vector.tensor_copy(out=gamma_col[:], in_=gamma_bf[:])
 
-        regroup_x_on_scalar(0, 0, 256)
-        regroup_x_on_gpsimd(0, 256, N)
+        regroup_x(SCALAR, 0, 0)
+        regroup_x(GPSIMD, 0, 1)
 
         w_grouped = const.tile([P, C, PACK], BF16, align_bytes=64)
         for u in range(PACK):
@@ -343,8 +338,8 @@ def tile_transformer_pa_t_kernel(tc, x, f, g, mask, Wv, gamma, out):
         )
         for q in range(PACK):
             scores(1, q)
-        regroup_x_on_scalar(1, 0, 256)
-        regroup_x_on_gpsimd(1, 256, N)
+        regroup_x(SCALAR, 1, 0)
+        regroup_x(GPSIMD, 1, 1)
 
         for r in range(B - 1):
             if on(r + 3):
@@ -400,8 +395,8 @@ def tile_transformer_pa_t_kernel(tc, x, f, g, mask, Wv, gamma, out):
                 copy_sum(r - 2, 2)
                 copy_sum(r - 2, 3)
             if on(r + 2):
-                for first in range(0, N, 256):
-                    regroup_x_on_gpsimd(r + 2, first, first + 256)
+                regroup_x(GPSIMD, r + 2, 0)
+                regroup_x(GPSIMD, r + 2, 1)
             if on(r - 1):
                 for w in range(2):
                     regroup_beta(r - 1, w)

@@ -17,7 +17,6 @@ PACK = 4
 EPS = 1e-6
 LEAKY_SLOPE = 0.2
 X_COLS_ON_SCALAR_AT_START = 256
-SCALAR, GPSIMD = 0, 1
 H, X = 0, 1
 
 FLOPS = B * (2 * C * C * N + 2 * CQ * N * N + 2 * C * N * N)
@@ -61,15 +60,21 @@ def tile_transformer_pa_t_kernel(tc, x, f, g, mask, Wv, gamma, out):
                 hx_grouped[k] = work.tile([P, 2, N, PACK], BF16, name="hx_grouped", tag="hx_grouped", align_bytes=64)
             return hx_grouped[k]
 
-        def regroup_x(engine, b, u):
-            source = x_rows[b][:, :, u * 2 * P : (u + 1) * 2 * P].rearrange("p t (q e) -> p e q t", e=2)
-            target = grouped(b - 1)[:, X, u * 2 * P : (u + 1) * 2 * P, :].rearrange("p (e q) t -> p e q t", e=2)
-            if engine == SCALAR:
-                nc.scalar.copy(out=target, in_=source)
-            else:
-                nc.gpsimd.tensor_scalar(
-                    out=target, in0=source, scalar1=1.0, scalar2=0.0, op0=ALU.mult, op1=ALU.add
-                )
+        def regroup_x_on_scalar(b, first, last):
+            nc.scalar.copy(
+                out=grouped(b - 1)[:, X, first:last, :].rearrange("p (c i) t -> p c t i", i=4),
+                in_=x_rows[b][:, :, first:last].rearrange("p t (c i) -> p c t i", i=4),
+            )
+
+        def regroup_x_on_gpsimd(b, first, last):
+            nc.gpsimd.tensor_scalar(
+                out=grouped(b - 1)[:, X, first:last, :],
+                in0=x_rows[b][:, :, first:last].rearrange("p t c -> p c t"),
+                scalar1=1.0,
+                scalar2=0.0,
+                op0=ALU.mult,
+                op1=ALU.add,
+            )
 
         def quantise_h_and_x(k):
             hx_codes[k] = work.tile([P, 2, N], U32, name="hx_codes", tag="hx_codes", align_bytes=64)
@@ -183,7 +188,10 @@ def tile_transformer_pa_t_kernel(tc, x, f, g, mask, Wv, gamma, out):
             if v % 2 == 0:
                 beta_ps[b, v // 2] = psum.tile([P, 2, 2, P], F32, name="beta_ps", tag="h_or_beta")
             nc.scalar.activation(
-                out=beta_t[b][:, v, :], in_=e_sb[b][:, v, :], func=ACT.Copy, scale=recip[b][:, v : v + 1]
+                out=beta_t[b][:, v, :].rearrange("p (u q e) -> p u q e", u=2, e=2),
+                in_=e_sb[b][:, v, :].rearrange("p (u e q) -> p u q e", u=2, e=2),
+                func=ACT.Copy,
+                scale=recip[b][:, v : v + 1],
             )
             words = beta_t[b][:, v, :].bitcast(F32)
             for u in range(2):
@@ -316,8 +324,8 @@ def tile_transformer_pa_t_kernel(tc, x, f, g, mask, Wv, gamma, out):
         gamma_col = const.tile([P, 1], F32)
         nc.vector.tensor_copy(out=gamma_col[:], in_=gamma_bf[:])
 
-        regroup_x(SCALAR, 0, 0)
-        regroup_x(GPSIMD, 0, 1)
+        regroup_x_on_scalar(0, 0, 256)
+        regroup_x_on_gpsimd(0, 256, N)
 
         w_grouped = const.tile([P, C, PACK], BF16, align_bytes=64)
         for u in range(PACK):
@@ -338,8 +346,8 @@ def tile_transformer_pa_t_kernel(tc, x, f, g, mask, Wv, gamma, out):
         )
         for q in range(PACK):
             scores(1, q)
-        regroup_x(SCALAR, 1, 0)
-        regroup_x(GPSIMD, 1, 1)
+        regroup_x_on_scalar(1, 0, 256)
+        regroup_x_on_gpsimd(1, 256, N)
 
         for r in range(B - 1):
             if on(r + 3):
@@ -395,8 +403,8 @@ def tile_transformer_pa_t_kernel(tc, x, f, g, mask, Wv, gamma, out):
                 copy_sum(r - 2, 2)
                 copy_sum(r - 2, 3)
             if on(r + 2):
-                regroup_x(GPSIMD, r + 2, 0)
-                regroup_x(GPSIMD, r + 2, 1)
+                for first in range(0, N, 256):
+                    regroup_x_on_gpsimd(r + 2, first, first + 256)
             if on(r - 1):
                 for w in range(2):
                     regroup_beta(r - 1, w)

@@ -17,6 +17,7 @@ PACK = 4
 EPS = 1e-6
 LEAKY_SLOPE = 0.2
 X_COLS_ON_SCALAR_AT_START = 256
+SCALAR, VECTOR = 0, 1
 H, X = 0, 1
 
 FLOPS = B * (2 * C * C * N + 2 * CQ * N * N + 2 * C * N * N)
@@ -66,6 +67,12 @@ def tile_transformer_pa_t_kernel(tc, x, f, g, mask, Wv, gamma, out):
                 in_=x_rows[b][:, :, first:last].rearrange("p t (c i) -> p c t i", i=4),
             )
 
+        def regroup_x_on_vector(b, first, last):
+            nc.vector.tensor_copy(
+                out=grouped(b - 1)[:, X, first:last, :].rearrange("p (c i) t -> p c t i", i=4),
+                in_=x_rows[b][:, :, first:last].rearrange("p t (c i) -> p c t i", i=4),
+            )
+
         def regroup_x_on_gpsimd(b, first, last):
             nc.gpsimd.tensor_scalar(
                 out=grouped(b - 1)[:, X, first:last, :],
@@ -100,8 +107,9 @@ def tile_transformer_pa_t_kernel(tc, x, f, g, mask, Wv, gamma, out):
                     stop=True,
                 )
 
-        def copy_h(b, u):
-            nc.scalar.copy(
+        def copy_h(engine, b, u):
+            copy = nc.scalar.copy if engine == SCALAR else nc.vector.tensor_copy
+            copy(
                 out=grouped(b + 1)[:, H, u * P : (u + 1) * P, :], in_=h_ps[b, u][:].rearrange("p t o -> p o t")
             )
 
@@ -182,28 +190,31 @@ def tile_transformer_pa_t_kernel(tc, x, f, g, mask, Wv, gamma, out):
             recip[b] = stats.tile([P, PACK], F32, name="recip", tag="recip")
             nc.vector.reciprocal(out=recip[b][:], in_=denom[b][:])
 
-        def normalise_and_transpose(b, v):
+        def normalise_and_transpose(engine, b, v):
             if v == 0:
                 beta_t[b] = work.tile([P, PACK, N], BF16, name="beta_t", tag="beta_t")
             if v % 2 == 0:
                 beta_ps[b, v // 2] = psum.tile([P, 2, 2, P], F32, name="beta_ps", tag="h_or_beta")
-            nc.scalar.activation(
-                out=beta_t[b][:, v, :].rearrange("p (u q e) -> p u q e", u=2, e=2),
-                in_=e_sb[b][:, v, :].rearrange("p (u e q) -> p u q e", u=2, e=2),
-                func=ACT.Copy,
-                scale=recip[b][:, v : v + 1],
-            )
+            pairs = beta_t[b][:, v, :].rearrange("p (u q e) -> p u q e", u=2, e=2)
+            values = e_sb[b][:, v, :].rearrange("p (u e q) -> p u q e", u=2, e=2)
+            if engine == SCALAR:
+                nc.scalar.activation(out=pairs, in_=values, func=ACT.Copy, scale=recip[b][:, v : v + 1])
+            else:
+                nc.vector.tensor_scalar(
+                    out=pairs, in0=values, scalar1=recip[b][:, v : v + 1], scalar2=None, op0=ALU.mult
+                )
             words = beta_t[b][:, v, :].bitcast(F32)
             for u in range(2):
                 nc.tensor.transpose(beta_ps[b, v // 2][:, v % 2, u, :], words[:, u * P : (u + 1) * P], identity[:])
 
-        def regroup_beta(b, w):
+        def regroup_beta(engine, b, w):
             if w == 0:
                 beta_grouped[b] = work.tile(
                     [P, N, PACK], BF16, name="beta_grouped", tag="beta_grouped", align_bytes=64
                 )
             words = beta_grouped[b][:, w * 2 * P : (w + 1) * 2 * P, :].rearrange("p n t -> p (n t)").bitcast(F32)
-            nc.scalar.copy(
+            copy = nc.scalar.copy if engine == SCALAR else nc.vector.tensor_copy
+            copy(
                 out=words.rearrange("p (v j u) -> p v j u", v=2, u=2),
                 in_=beta_ps[b, w][:].rearrange("p v u j -> p v j u"),
             )
@@ -260,14 +271,17 @@ def tile_transformer_pa_t_kernel(tc, x, f, g, mask, Wv, gamma, out):
                 scale=gamma_mask_cols[:, PACK * b + v : PACK * b + v + 1],
             )
 
+        def result_tile(b):
+            if b not in result:
+                result[b] = work.tile([P, PACK, N], F32, name="result", tag="result", bufs=3)
+            return result[b]
+
         def store(b, u):
             nc.sync.dma_start(out=out[b][u * P : (u + 1) * P, :], in_=result[b][:, u, :])
 
         def add_x(engine, b, u):
-            if u == 0:
-                result[b] = work.tile([P, PACK, N], F32, name="result", tag="result")
             engine.tensor_tensor(
-                out=result[b][:, u, :], in0=scaled[b][:, u, :], in1=x_rows[b][:, u, :], op=ALU.add
+                out=result_tile(b)[:, u, :], in0=scaled[b][:, u, :], in1=x_rows[b][:, u, :], op=ALU.add
             )
             store(b, u)
 
@@ -284,8 +298,9 @@ def tile_transformer_pa_t_kernel(tc, x, f, g, mask, Wv, gamma, out):
                     stop=v == PACK - 1,
                 )
 
-        def copy_sum(b, u):
-            nc.scalar.copy(out=result[b][:, u, :], in_=sum_ps[b, u][:])
+        def copy_sum(engine, b, u):
+            copy = nc.scalar.copy if engine == SCALAR else nc.vector.tensor_copy
+            copy(out=result_tile(b)[:, u, :], in_=sum_ps[b, u][:])
             store(b, u)
 
         def on(b):
@@ -358,13 +373,15 @@ def tile_transformer_pa_t_kernel(tc, x, f, g, mask, Wv, gamma, out):
                 for v in range(PACK):
                     exponential(r, v)
             for u in range(PACK):
-                copy_h(r, u)
+                copy_h(SCALAR, r, u)
             if on(r - 1):
                 mask_and_sum(r - 1, 0)
                 mask_and_sum(r - 1, 1)
             if on(r - 2):
                 quantise_beta(r - 2)
                 attend(r - 2)
+            if r > 0:
+                regroup_x_on_vector(r + 1, 0, 64)
             if on(r - 1):
                 mask_and_sum(r - 1, 2)
                 mask_and_sum(r - 1, 3)
@@ -398,16 +415,20 @@ def tile_transformer_pa_t_kernel(tc, x, f, g, mask, Wv, gamma, out):
                 add_x_in_psum(r - 2, 3)
             if on(r - 1):
                 for q in range(PACK):
-                    normalise_and_transpose(r - 1, q)
+                    normalise_and_transpose(SCALAR, r - 1, q)
             if on(r - 2):
-                copy_sum(r - 2, 2)
-                copy_sum(r - 2, 3)
+                copy_sum(SCALAR, r - 2, 2)
+                copy_sum(SCALAR, r - 2, 3)
             if on(r + 2):
-                for first in range(0, N, 256):
-                    regroup_x_on_gpsimd(r + 2, first, first + 256)
+                if r == 1:
+                    regroup_x_on_scalar(r + 2, 64, N)
+                else:
+                    regroup_x_on_scalar(r + 2, 64, 96)
+                    regroup_x_on_gpsimd(r + 2, 96, 304)
+                    regroup_x_on_gpsimd(r + 2, 304, 512)
             if on(r - 1):
                 for w in range(2):
-                    regroup_beta(r - 1, w)
+                    regroup_beta(SCALAR, r - 1, w)
             for v in range(PACK):
                 maximum(r + 1, v)
             for v in range(PACK):
@@ -415,67 +436,83 @@ def tile_transformer_pa_t_kernel(tc, x, f, g, mask, Wv, gamma, out):
             top(r + 1)
 
         w, z, y = B - 3, B - 2, B - 1
-        for u in range(PACK):
-            project(y, u)
+        project(y, 0)
+        project(y, 1)
+        project(y, 2)
+        project(y, 3)
         mask_and_sum(z, 0)
         mask_and_sum(z, 1)
-        quantise_beta(w)
-        attend(w)
         mask_and_sum(z, 2)
         mask_and_sum(z, 3)
-        quantise_h_and_x(y)
+        quantise_beta(w)
+        attend(w)
+        exponential(y, 0)
+        exponential(y, 1)
+        exponential(y, 2)
+        exponential(y, 3)
         denominator(z)
-        for v in range(PACK):
-            exponential(y, v)
-        for v in range(PACK):
-            scale_ot(w, v)
-        scale_o(w, 0)
+        quantise_h_and_x(y)
         reciprocal(z)
+        copy_h(SCALAR, y, 0)
+        copy_h(SCALAR, y, 1)
+        copy_h(SCALAR, y, 2)
+        copy_h(SCALAR, y, 3)
+        normalise_and_transpose(VECTOR, z, 0)
+        normalise_and_transpose(VECTOR, z, 1)
+        normalise_and_transpose(VECTOR, z, 2)
+        normalise_and_transpose(VECTOR, z, 3)
+        scale_ot(w, 0)
+        scale_ot(w, 1)
+        scale_ot(w, 2)
+        scale_ot(w, 3)
+        scale_o(w, 0)
         scale_o(w, 1)
-        add_x(nc.gpsimd, w, 0)
-        add_x(nc.vector, w, 1)
-        copy_h(y, 0)
-        copy_h(y, 1)
-        for q in range(PACK):
-            normalise_and_transpose(z, q)
-        copy_h(y, 2)
-        copy_h(y, 3)
-        for v in range(2):
-            regroup_beta(z, v)
-        for u in range(2, PACK):
-            add_x_in_psum(w, u)
-        for u in range(2, PACK):
-            copy_sum(w, u)
-        for v in range(PACK):
-            mask_and_sum(y, v)
+        regroup_beta(SCALAR, z, 0)
+        regroup_beta(SCALAR, z, 1)
+        add_x_in_psum(w, 2)
+        add_x_in_psum(w, 3)
+        copy_sum(SCALAR, w, 2)
+        copy_sum(SCALAR, w, 3)
+        mask_and_sum(y, 0)
+        mask_and_sum(y, 1)
+        mask_and_sum(y, 2)
+        mask_and_sum(y, 3)
         denominator(y)
         quantise_beta(z)
-        attend(z)
         reciprocal(y)
+        attend(z)
+        normalise_and_transpose(VECTOR, y, 0)
+        normalise_and_transpose(VECTOR, y, 1)
+        normalise_and_transpose(VECTOR, y, 2)
+        normalise_and_transpose(VECTOR, y, 3)
         quantise_h_and_x(B)
-        for q in range(PACK):
-            normalise_and_transpose(y, q)
-        for v in range(PACK):
-            scale_ot(z, v)
-        for v in range(2):
-            regroup_beta(y, v)
         scale_o(z, 0)
         scale_o(z, 1)
-        add_x(nc.gpsimd, z, 0)
-        add_x(nc.vector, z, 1)
-        for u in range(2, PACK):
-            add_x_in_psum(z, u)
-        for u in range(2, PACK):
-            copy_sum(z, u)
+        scale_ot(z, 0)
+        scale_ot(z, 1)
+        scale_ot(z, 2)
+        scale_ot(z, 3)
+        regroup_beta(SCALAR, y, 0)
+        regroup_beta(SCALAR, y, 1)
         quantise_beta(y)
         attend(y)
-        for v in range(PACK):
-            scale_ot(y, v)
+        add_x(nc.vector, w, 0)
+        add_x(nc.vector, w, 1)
+        scale_ot(y, 0)
+        scale_ot(y, 1)
+        scale_ot(y, 2)
+        scale_ot(y, 3)
+        add_x_in_psum(z, 2)
+        add_x_in_psum(z, 3)
         scale_o(y, 0)
         scale_o(y, 1)
-        add_x(nc.gpsimd, y, 0)
+        add_x(nc.gpsimd, z, 0)
+        add_x(nc.vector, y, 0)
         add_x(nc.vector, y, 1)
-        for u in range(2, PACK):
-            add_x_in_psum(y, u)
-        for u in range(2, PACK):
-            copy_sum(y, u)
+        add_x_in_psum(y, 2)
+        add_x_in_psum(y, 3)
+        copy_sum(SCALAR, z, 2)
+        copy_sum(SCALAR, z, 3)
+        add_x(nc.vector, z, 1)
+        copy_sum(SCALAR, y, 2)
+        copy_sum(VECTOR, y, 3)

@@ -17,8 +17,7 @@ PACK = 4
 EPS = 1e-6
 LEAKY_SLOPE = 0.2
 X_COLS_ON_SCALAR_AT_START = 256
-SCALAR, VECTOR = 0, 1
-H, X = 0, 1
+SCALAR, VECTOR, GPSIMD = 0, 1, 2
 
 FLOPS = B * (2 * C * C * N + 2 * CQ * N * N + 2 * C * N * N)
 
@@ -39,12 +38,13 @@ def tile_transformer_pa_t_kernel(tc, x, f, g, mask, Wv, gamma, out):
         loads = stack.enter_context(tc.tile_pool(name="loads", bufs=3))
         work = stack.enter_context(tc.tile_pool(name="work", bufs=2))
         stats = stack.enter_context(tc.tile_pool(name="stats", bufs=3))
-        psum = stack.enter_context(tc.psum_pool(name="psum", bufs=4))
+        psum = stack.enter_context(tc.psum_pool(name="psum", bufs=1))
 
         x_rows, f_sb, g_sb = {}, {}, {}
-        hx_grouped, hx_codes, hx_scales = {}, {}, {}
+        x_grouped, x_codes, x_scales = {}, {}, {}
+        h_grouped, h_codes, h_scales = {}, {}, {}
         h_ps, s_ps, neg_leaky, neg_s_max, neg_top = {}, {}, {}, {}, {}
-        e_sb, e_sum, em_sum, denom, recip = {}, {}, {}, {}, {}
+        e_sb, e_sum, em_sum, denom, recip, mask_ps = {}, {}, {}, {}, {}, {}
         beta_t, beta_ps, beta_grouped, beta_codes, beta_scales = {}, {}, {}, {}, {}
         o_ps, ot_ps, scaled, scaled_t, sum_ps, result = {}, {}, {}, {}, {}, {}
 
@@ -56,65 +56,58 @@ def tile_transformer_pa_t_kernel(tc, x, f, g, mask, Wv, gamma, out):
             x_rows[b] = loads.tile([P, PACK, N], BF16, name="x_rows", tag="x_rows", bufs=6)
             nc.sync.dma_start(out=x_rows[b][:], in_=x[b].rearrange("(t p) n -> p t n", p=P))
 
-        def grouped(k):
-            if k not in hx_grouped:
-                hx_grouped[k] = work.tile([P, 2, N, PACK], BF16, name="hx_grouped", tag="hx_grouped", align_bytes=64)
-            return hx_grouped[k]
+        def regroup_x(engine, b, first, last):
+            if b not in x_grouped:
+                tag = "x_grouped_1" if b == 1 else "x_grouped"
+                x_grouped[b] = work.tile([P, N, PACK], BF16, name="x_grouped", tag=tag, bufs=1, align_bytes=64)
+            if engine == SCALAR:
+                nc.scalar.copy(
+                    out=x_grouped[b][:, first:last, :].rearrange("p (c i) t -> p c t i", i=4),
+                    in_=x_rows[b][:, :, first:last].rearrange("p t (c i) -> p c t i", i=4),
+                )
+            else:
+                nc.gpsimd.tensor_scalar(
+                    out=x_grouped[b][:, first:last, :],
+                    in0=x_rows[b][:, :, first:last].rearrange("p t c -> p c t"),
+                    scalar1=1.0,
+                    scalar2=0.0,
+                    op0=ALU.mult,
+                    op1=ALU.add,
+                )
 
-        def regroup_x_on_scalar(b, first, last):
-            nc.scalar.copy(
-                out=grouped(b - 1)[:, X, first:last, :].rearrange("p (c i) t -> p c t i", i=4),
-                in_=x_rows[b][:, :, first:last].rearrange("p t (c i) -> p c t i", i=4),
-            )
+        def quantise_x(b):
+            x_codes[b] = work.tile([P, N], U32, name="x_codes", tag="x_codes", align_bytes=64)
+            x_scales[b] = work.tile([P, N], U8, name="x_scales", tag="x_scales", align_bytes=64)
+            quantise(nc, x_grouped[b], x_codes[b], x_scales[b])
 
-        def regroup_x_on_vector(b, first, last):
-            nc.vector.tensor_copy(
-                out=grouped(b - 1)[:, X, first:last, :].rearrange("p (c i) t -> p c t i", i=4),
-                in_=x_rows[b][:, :, first:last].rearrange("p t (c i) -> p c t i", i=4),
-            )
-
-        def regroup_x_on_gpsimd(b, first, last):
-            nc.gpsimd.tensor_scalar(
-                out=grouped(b - 1)[:, X, first:last, :],
-                in0=x_rows[b][:, :, first:last].rearrange("p t c -> p c t"),
-                scalar1=1.0,
-                scalar2=0.0,
-                op0=ALU.mult,
-                op1=ALU.add,
-            )
-
-        def quantise_h_and_x(k):
-            hx_codes[k] = work.tile([P, 2, N], U32, name="hx_codes", tag="hx_codes", align_bytes=64)
-            hx_scales[k] = work.tile([P, 2, N], U8, name="hx_scales", tag="hx_scales", align_bytes=64)
-            first = H if on(k - 1) else X
-            last = X if on(k + 1) else H
-            nc.vector.quantize_mx(
-                out=hx_codes[k][:, first : last + 1, :].rearrange("p s w -> p (s w)").bitcast(FP8X4),
-                scales=hx_scales[k][:, first : last + 1, :].rearrange("p s w -> p (s w)"),
-                in_=grouped(k)[:, first : last + 1, :, :].rearrange("p s w t -> p (s w t)"),
-            )
+        def quantise_h(b):
+            h_codes[b] = work.tile([P, N], U32, name="h_codes", tag="h_codes", align_bytes=64)
+            h_scales[b] = work.tile([P, N], U8, name="h_scales", tag="h_scales", align_bytes=64)
+            quantise(nc, h_grouped[b], h_codes[b], h_scales[b])
 
         def project(b, u):
-            h_ps[b, u] = psum.tile([P, PACK, P], F32, name="h_ps", tag="h_or_beta")
+            h_ps[b, u] = psum.tile([P, PACK, P], F32, name="h_ps", tag="h_or_beta", bufs=3)
             for t in range(PACK):
                 nc.tensor.matmul_mx(
                     out=h_ps[b, u][:, t, :],
-                    lhsT=hx_codes[b - 1][:, X, t * P : (t + 1) * P].bitcast(FP8X4),
-                    lhsT_scale=hx_scales[b - 1][:, X, t * P : (t + 1) * P],
+                    lhsT=x_codes[b][:, t * P : (t + 1) * P].bitcast(FP8X4),
+                    lhsT_scale=x_scales[b][:, t * P : (t + 1) * P],
                     rhs=w_codes[:, u * P : (u + 1) * P].bitcast(FP8X4),
                     rhs_scale=w_scales[:, u * P : (u + 1) * P],
                     start=True,
                     stop=True,
                 )
 
+        def copier(engine):
+            return nc.scalar.copy if engine == SCALAR else nc.vector.tensor_copy
+
         def copy_h(engine, b, u):
-            copy = nc.scalar.copy if engine == SCALAR else nc.vector.tensor_copy
-            copy(
-                out=grouped(b + 1)[:, H, u * P : (u + 1) * P, :], in_=h_ps[b, u][:].rearrange("p t o -> p o t")
-            )
+            if u == 0:
+                h_grouped[b] = work.tile([P, N, PACK], BF16, name="h_grouped", tag="h_grouped", align_bytes=64)
+            copier(engine)(out=h_grouped[b][:, u * P : (u + 1) * P, :], in_=h_ps[b, u][:].rearrange("p t o -> p o t"))
 
         def scores(b, v):
-            s_ps[b, v] = psum.tile([P, N], F32, name="s_ps", tag="s_or_o")
+            s_ps[b, v] = psum.tile([P, N], F32, name="s_ps", tag="s_or_o", bufs=4)
             nc.tensor.matmul(
                 out=s_ps[b, v][:], lhsT=g_sb[b][:, v * P : (v + 1) * P], rhs=f_sb[b][:], start=True, stop=True
             )
@@ -167,6 +160,12 @@ def tile_transformer_pa_t_kernel(tc, x, f, g, mask, Wv, gamma, out):
                 accum_out=e_sum[b][:, v : v + 1],
             )
 
+        def spread_mask(b):
+            mask_ps[b] = psum.tile([P, N], F32, name="mask_ps", tag="mask", bufs=1)
+            for t in range(PACK):
+                column = mask_cols[:, PACK * b + t : PACK * b + t + 1]
+                nc.tensor.transpose(mask_ps[b][:, t * P : (t + 1) * P], column.to_broadcast([P, P]), identity[:])
+
         def mask_and_sum(b, v):
             if v == 0:
                 em_sum[b] = stats.tile([P, PACK], F32, name="em_sum", tag="em_sum")
@@ -174,7 +173,7 @@ def tile_transformer_pa_t_kernel(tc, x, f, g, mask, Wv, gamma, out):
                 out=e_sb[b][:, v, :],
                 in0=e_sb[b][:, v, :],
                 scalar=1.0,
-                in1=mask_rows[:, b, :],
+                in1=mask_ps[b][:] if b in mask_ps else mask_rows[:, b, :],
                 op0=ALU.mult,
                 op1=ALU.mult,
                 accum_out=em_sum[b][:, v : v + 1],
@@ -190,19 +189,25 @@ def tile_transformer_pa_t_kernel(tc, x, f, g, mask, Wv, gamma, out):
             recip[b] = stats.tile([P, PACK], F32, name="recip", tag="recip")
             nc.vector.reciprocal(out=recip[b][:], in_=denom[b][:])
 
-        def normalise_and_transpose(engine, b, v):
-            if v == 0:
+        def normalise(engine, b, v):
+            if b not in beta_t:
                 beta_t[b] = work.tile([P, PACK, N], BF16, name="beta_t", tag="beta_t")
-            if v % 2 == 0:
-                beta_ps[b, v // 2] = psum.tile([P, 2, 2, P], F32, name="beta_ps", tag="h_or_beta")
             pairs = beta_t[b][:, v, :].rearrange("p (u q e) -> p u q e", u=2, e=2)
             values = e_sb[b][:, v, :].rearrange("p (u e q) -> p u q e", u=2, e=2)
             if engine == SCALAR:
                 nc.scalar.activation(out=pairs, in_=values, func=ACT.Copy, scale=recip[b][:, v : v + 1])
-            else:
+            elif engine == VECTOR:
                 nc.vector.tensor_scalar(
                     out=pairs, in0=values, scalar1=recip[b][:, v : v + 1], scalar2=None, op0=ALU.mult
                 )
+            else:
+                nc.gpsimd.tensor_scalar(
+                    out=pairs, in0=values, scalar1=recip[b][:, v : v + 1], scalar2=0.0, op0=ALU.mult, op1=ALU.add
+                )
+
+        def transpose_beta(b, v):
+            if v % 2 == 0:
+                beta_ps[b, v // 2] = psum.tile([P, 2, 2, P], F32, name="beta_ps", tag="h_or_beta", bufs=3)
             words = beta_t[b][:, v, :].bitcast(F32)
             for u in range(2):
                 nc.tensor.transpose(beta_ps[b, v // 2][:, v % 2, u, :], words[:, u * P : (u + 1) * P], identity[:])
@@ -227,22 +232,22 @@ def tile_transformer_pa_t_kernel(tc, x, f, g, mask, Wv, gamma, out):
         def attend(b):
             for v in range(PACK):
                 if v % 2 == 0:
-                    ot_ps[b, v // 2] = psum.tile([P, 2, 2 * P], F32, name="ot_ps", tag="s_or_o")
+                    ot_ps[b, v // 2] = psum.tile([P, 2, 2 * P], F32, name="ot_ps", tag="s_or_o", bufs=4)
                 nc.tensor.matmul_mx(
                     out=ot_ps[b, v // 2][:, v % 2, :],
                     lhsT=beta_codes[b][:, v * P : (v + 1) * P].bitcast(FP8X4),
                     lhsT_scale=beta_scales[b][:, v * P : (v + 1) * P],
-                    rhs=hx_codes[b + 1][:, H, 2 * P :].bitcast(FP8X4),
-                    rhs_scale=hx_scales[b + 1][:, H, 2 * P :],
+                    rhs=h_codes[b][:, 2 * P :].bitcast(FP8X4),
+                    rhs_scale=h_scales[b][:, 2 * P :],
                     start=True,
                     stop=True,
                 )
             for u in range(2):
-                o_ps[b, u] = psum.tile([P, N], F32, name="o_ps", tag="s_or_o")
+                o_ps[b, u] = psum.tile([P, N], F32, name="o_ps", tag="s_or_o", bufs=4)
                 nc.tensor.matmul_mx(
                     out=o_ps[b, u][:],
-                    lhsT=hx_codes[b + 1][:, H, u * P : (u + 1) * P].bitcast(FP8X4),
-                    lhsT_scale=hx_scales[b + 1][:, H, u * P : (u + 1) * P],
+                    lhsT=h_codes[b][:, u * P : (u + 1) * P].bitcast(FP8X4),
+                    lhsT_scale=h_scales[b][:, u * P : (u + 1) * P],
                     rhs=beta_codes[b][:].bitcast(FP8X4),
                     rhs_scale=beta_scales[b][:],
                     start=True,
@@ -286,7 +291,7 @@ def tile_transformer_pa_t_kernel(tc, x, f, g, mask, Wv, gamma, out):
             store(b, u)
 
         def add_x_in_psum(b, u):
-            sum_ps[b, u] = psum.tile([P, N], F32, name="sum_ps", tag="h_or_beta")
+            sum_ps[b, u] = psum.tile([P, N], F32, name="sum_ps", tag="h_or_beta", bufs=3)
             nc.tensor.matmul(out=sum_ps[b, u][:], lhsT=identity_bf[:], rhs=x_rows[b][:, u, :], start=True, stop=False)
             for v in range(PACK):
                 nc.tensor.matmul(
@@ -338,154 +343,174 @@ def tile_transformer_pa_t_kernel(tc, x, f, g, mask, Wv, gamma, out):
 
         gamma_col = const.tile([P, 1], F32)
         nc.vector.tensor_copy(out=gamma_col[:], in_=gamma_bf[:])
-
-        regroup_x_on_scalar(0, 0, 256)
-        regroup_x_on_gpsimd(0, 256, N)
-
+        regroup_x(SCALAR, 0, 0, 320)
+        regroup_x(GPSIMD, 0, 320, N)
         w_grouped = const.tile([P, C, PACK], BF16, align_bytes=64)
         for u in range(PACK):
-            w_t = psum.tile([P, PACK, P], BF16, name="w_t", tag="h_or_beta")
+            w_t = psum.tile([P, PACK, P], BF16, name="w_t", tag="h_or_beta", bufs=3)
             for t in range(PACK):
                 nc.tensor.transpose(w_t[:, t, :], w_rows[:, u, t * P : (t + 1) * P], identity_bf[:])
             nc.scalar.copy(out=w_grouped[:, u * P : (u + 1) * P, :], in_=w_t[:].rearrange("p t o -> p o t"))
         w_codes = const.tile([P, C], U32, align_bytes=64)
         w_scales = const.tile([P, C], U8, align_bytes=64)
+        quantise_x(0)
         quantise(nc, w_grouped, w_codes, w_scales)
-        quantise_h_and_x(-1)
-
-        mask_t = psum.tile([P, P], BF16, name="mask_t", tag="h_or_beta")
-        nc.tensor.transpose(mask_t[:], mask_tiles[:], identity_bf[:])
-        gamma_mask_cols = const.tile([P, B * PACK], F32)
-        nc.vector.tensor_scalar(
-            out=gamma_mask_cols[:], in0=mask_t[:, : B * PACK], scalar1=gamma_col[:, 0:1], scalar2=None, op0=ALU.mult
-        )
         for q in range(PACK):
             scores(1, q)
-        regroup_x_on_scalar(1, 0, 256)
-        regroup_x_on_gpsimd(1, 256, N)
+        regroup_x(GPSIMD, 1, 256, N)
+        regroup_x(SCALAR, 1, 0, 256)
+        quantise_x(1)
+        for v in range(PACK):
+            exponential(0, v)
+        mask_t = psum.tile([P, P], BF16, name="mask_t", tag="mask", bufs=1)
+        nc.tensor.transpose(mask_t[:], mask_tiles[:], identity_bf[:])
+        mask_cols = const.tile([P, B * PACK], F32)
+        nc.scalar.copy(out=mask_cols[:], in_=mask_t[:, : B * PACK])
+        gamma_mask_cols = const.tile([P, B * PACK], F32)
+        nc.scalar.activation(
+            out=gamma_mask_cols[:], in_=mask_t[:, : B * PACK], func=ACT.Copy, scale=gamma_col[:, 0:1]
+        )
+        spread_mask(0)
 
+        project(0, 0)
+        project(0, 1)
+        project(0, 2)
         for r in range(B - 1):
             if on(r + 3):
                 load(r + 3)
-            for u in range(PACK):
-                project(r, u)
+            copy_h(SCALAR, r, 0)
+            project(r, 3)
+            copy_h(SCALAR, r, 1)
+            copy_h(SCALAR, r, 2)
+            copy_h(SCALAR, r, 3)
             if r == 0:
                 for v in range(PACK):
-                    exponential(r, v)
-            for u in range(PACK):
-                copy_h(SCALAR, r, u)
-            if on(r - 1):
-                mask_and_sum(r - 1, 0)
-                mask_and_sum(r - 1, 1)
+                    maximum(1, v)
             if on(r - 2):
                 quantise_beta(r - 2)
                 attend(r - 2)
             if r > 0:
-                regroup_x_on_vector(r + 1, 0, 64)
-            if on(r - 1):
-                mask_and_sum(r - 1, 2)
-                mask_and_sum(r - 1, 3)
-            quantise_h_and_x(r)
-            if on(r - 1):
-                denominator(r - 1)
+                quantise_x(r + 1)
             if r > 0:
-                exponential(r, 0)
+                mask_and_sum(r - 1, 0)
+            if on(r + 2):
+                regroup_x(GPSIMD, r + 2, 0, 160)
+                regroup_x(GPSIMD, r + 2, 160, 320)
+            if r > 0:
+                for v in range(1, PACK):
+                    mask_and_sum(r - 1, v)
+                quantise_h(r - 1)
+                denominator(r - 1)
             if on(r - 2):
                 for v in range(PACK):
                     scale_ot(r - 2, v)
                     if v % 2 == 1:
                         scores(r + 1, v // 2)
+                add_x_in_psum(r - 2, 2)
+                add_x_in_psum(r - 2, 3)
                 scale_o(r - 2, 0)
-            if on(r - 1):
-                reciprocal(r - 1)
-            if on(r - 2):
                 scores(r + 1, 2)
-                scale_o(r - 2, 1)
-                scores(r + 1, 3)
-                add_x(nc.gpsimd, r - 2, 0)
-                add_x(nc.gpsimd, r - 2, 1)
             elif r == 1:
                 for q in range(PACK):
                     scores(r + 1, q)
             if r > 0:
-                for v in range(1, PACK):
-                    exponential(r, v)
+                reciprocal(r - 1)
             if on(r - 2):
-                add_x_in_psum(r - 2, 2)
-                add_x_in_psum(r - 2, 3)
-            if on(r - 1):
-                for q in range(PACK):
-                    normalise_and_transpose(SCALAR, r - 1, q)
+                scale_o(r - 2, 1)
+                scores(r + 1, 3)
+            if r > 0:
+                spread_mask(r)
+                for v in range(PACK):
+                    exponential(r, v)
+                for v in range(3, PACK):
+                    normalise(GPSIMD, r - 1, v)
+            if on(r - 2):
+                add_x(nc.gpsimd, r - 2, 0)
+                add_x(nc.gpsimd, r - 2, 1)
+            if r > 0:
+                normalise(SCALAR, r - 1, 0)
+                normalise(SCALAR, r - 1, 1)
+                transpose_beta(r - 1, 0)
+                transpose_beta(r - 1, 1)
             if on(r - 2):
                 copy_sum(SCALAR, r - 2, 2)
+            if r > 0:
+                for v in range(2, 3):
+                    normalise(SCALAR, r - 1, v)
+                transpose_beta(r - 1, 2)
+                transpose_beta(r - 1, 3)
+            if on(r - 2):
                 copy_sum(SCALAR, r - 2, 3)
             if on(r + 2):
-                if r == 1:
-                    regroup_x_on_scalar(r + 2, 64, N)
-                else:
-                    regroup_x_on_scalar(r + 2, 64, 96)
-                    regroup_x_on_gpsimd(r + 2, 96, 304)
-                    regroup_x_on_gpsimd(r + 2, 304, 512)
-            if on(r - 1):
-                for w in range(2):
-                    regroup_beta(SCALAR, r - 1, w)
-            for v in range(PACK):
-                maximum(r + 1, v)
+                regroup_x(GPSIMD, r + 2, 320, 416)
+                regroup_x(GPSIMD, r + 2, 416, 512)
+            if r > 0:
+                regroup_beta(SCALAR, r - 1, 0)
+                regroup_beta(SCALAR, r - 1, 1)
+                for v in range(PACK):
+                    maximum(r + 1, v)
+            for u in range(3):
+                project(r + 1, u)
             for v in range(PACK):
                 leaky(r + 1, v)
             top(r + 1)
 
         w, z, y = B - 3, B - 2, B - 1
-        project(y, 0)
-        project(y, 1)
-        project(y, 2)
+        copy_h(SCALAR, y, 0)
         project(y, 3)
+        quantise_beta(w)
+        attend(w)
         mask_and_sum(z, 0)
         mask_and_sum(z, 1)
         mask_and_sum(z, 2)
         mask_and_sum(z, 3)
-        quantise_beta(w)
-        attend(w)
         exponential(y, 0)
         exponential(y, 1)
         exponential(y, 2)
         exponential(y, 3)
-        denominator(z)
-        quantise_h_and_x(y)
-        reciprocal(z)
-        copy_h(SCALAR, y, 0)
         copy_h(SCALAR, y, 1)
         copy_h(SCALAR, y, 2)
-        copy_h(SCALAR, y, 3)
-        normalise_and_transpose(VECTOR, z, 0)
-        normalise_and_transpose(VECTOR, z, 1)
-        normalise_and_transpose(VECTOR, z, 2)
-        normalise_and_transpose(VECTOR, z, 3)
+        denominator(z)
+        quantise_h(z)
         scale_ot(w, 0)
         scale_ot(w, 1)
         scale_ot(w, 2)
         scale_ot(w, 3)
         scale_o(w, 0)
+        reciprocal(z)
         scale_o(w, 1)
-        regroup_beta(SCALAR, z, 0)
-        regroup_beta(SCALAR, z, 1)
         add_x_in_psum(w, 2)
         add_x_in_psum(w, 3)
+        copy_h(SCALAR, y, 3)
         copy_sum(SCALAR, w, 2)
+        normalise(VECTOR, z, 0)
+        transpose_beta(z, 0)
+        normalise(VECTOR, z, 1)
+        transpose_beta(z, 1)
+        normalise(VECTOR, z, 2)
+        transpose_beta(z, 2)
+        normalise(VECTOR, z, 3)
+        transpose_beta(z, 3)
+        regroup_beta(SCALAR, z, 0)
+        regroup_beta(SCALAR, z, 1)
         copy_sum(SCALAR, w, 3)
         mask_and_sum(y, 0)
         mask_and_sum(y, 1)
         mask_and_sum(y, 2)
         mask_and_sum(y, 3)
-        denominator(y)
         quantise_beta(z)
-        reciprocal(y)
         attend(z)
-        normalise_and_transpose(VECTOR, y, 0)
-        normalise_and_transpose(VECTOR, y, 1)
-        normalise_and_transpose(VECTOR, y, 2)
-        normalise_and_transpose(VECTOR, y, 3)
-        quantise_h_and_x(B)
+        denominator(y)
+        quantise_h(y)
+        reciprocal(y)
+        normalise(VECTOR, y, 0)
+        transpose_beta(y, 0)
+        normalise(VECTOR, y, 1)
+        transpose_beta(y, 1)
+        normalise(VECTOR, y, 2)
+        transpose_beta(y, 2)
+        normalise(VECTOR, y, 3)
+        transpose_beta(y, 3)
         scale_o(z, 0)
         scale_o(z, 1)
         scale_ot(z, 0)
@@ -510,9 +535,9 @@ def tile_transformer_pa_t_kernel(tc, x, f, g, mask, Wv, gamma, out):
         add_x(nc.vector, y, 0)
         add_x(nc.vector, y, 1)
         add_x_in_psum(y, 2)
-        add_x_in_psum(y, 3)
         copy_sum(SCALAR, z, 2)
         copy_sum(SCALAR, z, 3)
+        add_x_in_psum(y, 3)
         add_x(nc.vector, z, 1)
         copy_sum(SCALAR, y, 2)
         copy_sum(VECTOR, y, 3)

@@ -308,6 +308,19 @@ def tile_transformer_pa_t_kernel(tc, x, f, g, mask, Wv, gamma, out):
             copy(out=result_tile(b)[:, u, :], in_=sum_ps[b, u][:])
             store(b, u)
 
+        def warm_up(b, n):
+            dummy = psum.tile([P, N], F32, name="dummy", tag="mask", bufs=1)
+            for i in range(n):
+                nc.tensor.matmul_mx(
+                    out=dummy[:],
+                    lhsT=w_codes[:, :P].bitcast(FP8X4),
+                    lhsT_scale=w_scales[:, :P],
+                    rhs=h_codes[b][:].bitcast(FP8X4),
+                    rhs_scale=h_scales[b][:],
+                    start=True,
+                    stop=True,
+                )
+
         def on(b):
             return 0 <= b < B
 
@@ -518,7 +531,8 @@ def tile_transformer_pa_t_kernel(tc, x, f, g, mask, Wv, gamma, out):
         scale_ot(z, 2)
         scale_ot(z, 3)
         regroup_beta(SCALAR, y, 0)
-        regroup_beta(SCALAR, y, 1)
+        regroup_beta(VECTOR, y, 1)
+        warm_up(z, 3)
         quantise_beta(y)
         attend(y)
         add_x(nc.vector, w, 0)

@@ -290,9 +290,11 @@ def tile_transformer_pa_t_kernel(tc, x, f, g, mask, Wv, gamma, out):
             )
             store(b, u)
 
-        def add_x_in_psum(b, u):
+        def put_x(b, u):
             sum_ps[b, u] = psum.tile([P, N], F32, name="sum_ps", tag="h_or_beta", bufs=3)
             nc.tensor.matmul(out=sum_ps[b, u][:], lhsT=identity_bf[:], rhs=x_rows[b][:, u, :], start=True, stop=False)
+
+        def add_scaled(b, u):
             for v in range(PACK):
                 nc.tensor.matmul(
                     out=sum_ps[b, u][:, v * P : (v + 1) * P],
@@ -303,23 +305,14 @@ def tile_transformer_pa_t_kernel(tc, x, f, g, mask, Wv, gamma, out):
                     stop=v == PACK - 1,
                 )
 
+        def add_x_in_psum(b, u):
+            put_x(b, u)
+            add_scaled(b, u)
+
         def copy_sum(engine, b, u):
             copy = nc.scalar.copy if engine == SCALAR else nc.vector.tensor_copy
             copy(out=result_tile(b)[:, u, :], in_=sum_ps[b, u][:])
             store(b, u)
-
-        def warm_up(b, n):
-            dummy = psum.tile([P, N], F32, name="dummy", tag="mask", bufs=1)
-            for i in range(n):
-                nc.tensor.matmul_mx(
-                    out=dummy[:],
-                    lhsT=w_codes[:, :P].bitcast(FP8X4),
-                    lhsT_scale=w_scales[:, :P],
-                    rhs=h_codes[b][:].bitcast(FP8X4),
-                    rhs_scale=h_scales[b][:],
-                    start=True,
-                    stop=True,
-                )
 
         def on(b):
             return 0 <= b < B
@@ -407,8 +400,8 @@ def tile_transformer_pa_t_kernel(tc, x, f, g, mask, Wv, gamma, out):
             if r > 0:
                 mask_and_sum(r - 1, 0)
             if on(r + 2):
-                regroup_x(GPSIMD, r + 2, 0, 160)
-                regroup_x(GPSIMD, r + 2, 160, 320)
+                regroup_x(GPSIMD, r + 2, 0, 152)
+                regroup_x(GPSIMD, r + 2, 152, 304)
             if r > 0:
                 for v in range(1, PACK):
                     mask_and_sum(r - 1, v)
@@ -419,11 +412,15 @@ def tile_transformer_pa_t_kernel(tc, x, f, g, mask, Wv, gamma, out):
                     scale_ot(r - 2, v)
                     if v % 2 == 1:
                         scores(r + 1, v // 2)
-                add_x_in_psum(r - 2, 2)
-                add_x_in_psum(r - 2, 3)
+                put_x(r - 2, 2)
+                put_x(r - 2, 3)
+                add_scaled(r - 2, 2)
+                add_scaled(r - 2, 3)
+                spread_mask(r)
                 scale_o(r - 2, 0)
                 scores(r + 1, 2)
             elif r == 1:
+                spread_mask(r)
                 for q in range(PACK):
                     scores(r + 1, q)
             if r > 0:
@@ -432,8 +429,7 @@ def tile_transformer_pa_t_kernel(tc, x, f, g, mask, Wv, gamma, out):
                 scale_o(r - 2, 1)
                 scores(r + 1, 3)
             if r > 0:
-                spread_mask(r)
-                for v in range(PACK):
+                for v in range(3):
                     exponential(r, v)
                 for v in range(3, PACK):
                     normalise(GPSIMD, r - 1, v)
@@ -441,22 +437,22 @@ def tile_transformer_pa_t_kernel(tc, x, f, g, mask, Wv, gamma, out):
                 add_x(nc.gpsimd, r - 2, 0)
                 add_x(nc.gpsimd, r - 2, 1)
             if r > 0:
-                normalise(SCALAR, r - 1, 0)
-                normalise(SCALAR, r - 1, 1)
+                for v in range(3):
+                    normalise(SCALAR, r - 1, v)
                 transpose_beta(r - 1, 0)
                 transpose_beta(r - 1, 1)
             if on(r - 2):
                 copy_sum(SCALAR, r - 2, 2)
             if r > 0:
-                for v in range(2, 3):
-                    normalise(SCALAR, r - 1, v)
                 transpose_beta(r - 1, 2)
                 transpose_beta(r - 1, 3)
             if on(r - 2):
                 copy_sum(SCALAR, r - 2, 3)
+            if r > 0:
+                for v in range(3, PACK):
+                    exponential(r, v)
             if on(r + 2):
-                regroup_x(GPSIMD, r + 2, 320, 416)
-                regroup_x(GPSIMD, r + 2, 416, 512)
+                regroup_x(GPSIMD, r + 2, 304, 512)
             if r > 0:
                 regroup_beta(SCALAR, r - 1, 0)
                 regroup_beta(SCALAR, r - 1, 1)
@@ -492,8 +488,10 @@ def tile_transformer_pa_t_kernel(tc, x, f, g, mask, Wv, gamma, out):
         scale_o(w, 0)
         reciprocal(z)
         scale_o(w, 1)
-        add_x_in_psum(w, 2)
-        add_x_in_psum(w, 3)
+        put_x(w, 2)
+        put_x(w, 3)
+        add_scaled(w, 2)
+        add_scaled(w, 3)
         copy_h(SCALAR, y, 3)
         copy_sum(SCALAR, w, 2)
         normalise(VECTOR, z, 0)
@@ -532,24 +530,25 @@ def tile_transformer_pa_t_kernel(tc, x, f, g, mask, Wv, gamma, out):
         scale_ot(z, 3)
         regroup_beta(SCALAR, y, 0)
         regroup_beta(VECTOR, y, 1)
-        warm_up(z, 3)
+        put_x(z, 2)
+        put_x(z, 3)
+        add_scaled(z, 2)
+        add_scaled(z, 3)
         quantise_beta(y)
         attend(y)
         add_x(nc.vector, w, 0)
         add_x(nc.vector, w, 1)
+        copy_sum(SCALAR, z, 2)
         scale_ot(y, 0)
         scale_ot(y, 1)
         scale_ot(y, 2)
         scale_ot(y, 3)
-        add_x_in_psum(z, 2)
-        add_x_in_psum(z, 3)
         scale_o(y, 0)
         scale_o(y, 1)
         add_x(nc.gpsimd, z, 0)
         add_x(nc.vector, y, 0)
         add_x(nc.vector, y, 1)
         add_x_in_psum(y, 2)
-        copy_sum(SCALAR, z, 2)
         copy_sum(SCALAR, z, 3)
         add_x_in_psum(y, 3)
         add_x(nc.vector, z, 1)

@@ -14,10 +14,11 @@ ACT = mybir.ActivationFunctionType
 B, C, CQ, N = 16, 512, 128, 512
 P = 128
 PACK = 4
+HALF = 256
 EPS = 1e-6
 LEAKY_SLOPE = 0.2
-X_COLS_ON_SCALAR_AT_START = 256
-SCALAR, VECTOR, GPSIMD = 0, 1, 2
+X_COLS_FIRST = 288
+SCALAR, VECTOR, GPSIMD = "scalar", "vector", "gpsimd"
 
 FLOPS = B * (2 * C * C * N + 2 * CQ * N * N + 2 * C * N * N)
 
@@ -42,11 +43,17 @@ def tile_transformer_pa_t_kernel(tc, x, f, g, mask, Wv, gamma, out):
 
         x_rows, f_sb, g_sb = {}, {}, {}
         x_grouped, x_codes, x_scales = {}, {}, {}
-        h_grouped, h_codes, h_scales = {}, {}, {}
-        h_ps, s_ps, neg_leaky, neg_s_max, neg_top = {}, {}, {}, {}, {}
-        e_sb, e_sum, em_sum, denom, recip, mask_ps = {}, {}, {}, {}, {}, {}
+        h_ps, h_grouped, h_codes, h_scales = {}, {}, {}, {}
+        s_ps, neg_leaky, neg_s_max, neg_top = {}, {}, {}, {}
+        e_sb, e_sum, mask_ps, em_sum, denom, recip = {}, {}, {}, {}, {}, {}
         beta_t, beta_ps, beta_grouped, beta_codes, beta_scales = {}, {}, {}, {}, {}
         o_ps, ot_ps, scaled, scaled_t, sum_ps, result = {}, {}, {}, {}, {}, {}
+
+        def copy(engine, out, in_):
+            if engine == SCALAR:
+                nc.scalar.copy(out=out, in_=in_)
+            else:
+                nc.vector.tensor_copy(out=out, in_=in_)
 
         def load(b):
             f_sb[b] = loads.tile([P, N], BF16, name="f_sb", tag="f_sb")
@@ -80,11 +87,6 @@ def tile_transformer_pa_t_kernel(tc, x, f, g, mask, Wv, gamma, out):
             x_scales[b] = work.tile([P, N], U8, name="x_scales", tag="x_scales", align_bytes=64)
             quantise(nc, x_grouped[b], x_codes[b], x_scales[b])
 
-        def quantise_h(b):
-            h_codes[b] = work.tile([P, N], U32, name="h_codes", tag="h_codes", align_bytes=64)
-            h_scales[b] = work.tile([P, N], U8, name="h_scales", tag="h_scales", align_bytes=64)
-            quantise(nc, h_grouped[b], h_codes[b], h_scales[b])
-
         def project(b, u):
             h_ps[b, u] = psum.tile([P, PACK, P], F32, name="h_ps", tag="h_or_beta", bufs=3)
             for t in range(PACK):
@@ -98,13 +100,17 @@ def tile_transformer_pa_t_kernel(tc, x, f, g, mask, Wv, gamma, out):
                     stop=True,
                 )
 
-        def copier(engine):
-            return nc.scalar.copy if engine == SCALAR else nc.vector.tensor_copy
-
-        def copy_h(engine, b, u):
+        def copy_h(b, u):
             if u == 0:
                 h_grouped[b] = work.tile([P, N, PACK], BF16, name="h_grouped", tag="h_grouped", align_bytes=64)
-            copier(engine)(out=h_grouped[b][:, u * P : (u + 1) * P, :], in_=h_ps[b, u][:].rearrange("p t o -> p o t"))
+            nc.scalar.copy(
+                out=h_grouped[b][:, u * P : (u + 1) * P, :], in_=h_ps[b, u][:].rearrange("p t o -> p o t")
+            )
+
+        def quantise_h(b):
+            h_codes[b] = work.tile([P, N], U32, name="h_codes", tag="h_codes", align_bytes=64)
+            h_scales[b] = work.tile([P, N], U8, name="h_scales", tag="h_scales", align_bytes=64)
+            quantise(nc, h_grouped[b], h_codes[b], h_scales[b])
 
         def scores(b, v):
             s_ps[b, v] = psum.tile([P, N], F32, name="s_ps", tag="s_or_o", bufs=4)
@@ -166,14 +172,14 @@ def tile_transformer_pa_t_kernel(tc, x, f, g, mask, Wv, gamma, out):
                 column = mask_cols[:, PACK * b + t : PACK * b + t + 1]
                 nc.tensor.transpose(mask_ps[b][:, t * P : (t + 1) * P], column.to_broadcast([P, P]), identity[:])
 
-        def mask_and_sum(b, v):
+        def mask_and_sum(b, v, mask_row):
             if v == 0:
                 em_sum[b] = stats.tile([P, PACK], F32, name="em_sum", tag="em_sum")
             nc.vector.scalar_tensor_tensor(
                 out=e_sb[b][:, v, :],
                 in0=e_sb[b][:, v, :],
                 scalar=1.0,
-                in1=mask_ps[b][:] if b in mask_ps else mask_rows[:, b, :],
+                in1=mask_row,
                 op0=ALU.mult,
                 op1=ALU.mult,
                 accum_out=em_sum[b][:, v : v + 1],
@@ -193,16 +199,15 @@ def tile_transformer_pa_t_kernel(tc, x, f, g, mask, Wv, gamma, out):
             if b not in beta_t:
                 beta_t[b] = work.tile([P, PACK, N], BF16, name="beta_t", tag="beta_t")
             pairs = beta_t[b][:, v, :].rearrange("p (u q e) -> p u q e", u=2, e=2)
-            values = e_sb[b][:, v, :].rearrange("p (u e q) -> p u q e", u=2, e=2)
+            em = e_sb[b][:, v, :].rearrange("p (u e q) -> p u q e", u=2, e=2)
+            factor = recip[b][:, v : v + 1]
             if engine == SCALAR:
-                nc.scalar.activation(out=pairs, in_=values, func=ACT.Copy, scale=recip[b][:, v : v + 1])
+                nc.scalar.activation(out=pairs, in_=em, func=ACT.Copy, scale=factor)
             elif engine == VECTOR:
-                nc.vector.tensor_scalar(
-                    out=pairs, in0=values, scalar1=recip[b][:, v : v + 1], scalar2=None, op0=ALU.mult
-                )
+                nc.vector.tensor_scalar(out=pairs, in0=em, scalar1=factor, scalar2=None, op0=ALU.mult)
             else:
                 nc.gpsimd.tensor_scalar(
-                    out=pairs, in0=values, scalar1=recip[b][:, v : v + 1], scalar2=0.0, op0=ALU.mult, op1=ALU.add
+                    out=pairs, in0=em, scalar1=factor, scalar2=0.0, op0=ALU.mult, op1=ALU.add
                 )
 
         def transpose_beta(b, v):
@@ -218,10 +223,10 @@ def tile_transformer_pa_t_kernel(tc, x, f, g, mask, Wv, gamma, out):
                     [P, N, PACK], BF16, name="beta_grouped", tag="beta_grouped", align_bytes=64
                 )
             words = beta_grouped[b][:, w * 2 * P : (w + 1) * 2 * P, :].rearrange("p n t -> p (n t)").bitcast(F32)
-            copy = nc.scalar.copy if engine == SCALAR else nc.vector.tensor_copy
             copy(
-                out=words.rearrange("p (v j u) -> p v j u", v=2, u=2),
-                in_=beta_ps[b, w][:].rearrange("p v u j -> p v j u"),
+                engine,
+                words.rearrange("p (v j u) -> p v j u", v=2, u=2),
+                beta_ps[b, w][:].rearrange("p v u j -> p v j u"),
             )
 
         def quantise_beta(b):
@@ -232,13 +237,13 @@ def tile_transformer_pa_t_kernel(tc, x, f, g, mask, Wv, gamma, out):
         def attend(b):
             for v in range(PACK):
                 if v % 2 == 0:
-                    ot_ps[b, v // 2] = psum.tile([P, 2, 2 * P], F32, name="ot_ps", tag="s_or_o", bufs=4)
+                    ot_ps[b, v // 2] = psum.tile([P, 2, HALF], F32, name="ot_ps", tag="s_or_o", bufs=4)
                 nc.tensor.matmul_mx(
                     out=ot_ps[b, v // 2][:, v % 2, :],
                     lhsT=beta_codes[b][:, v * P : (v + 1) * P].bitcast(FP8X4),
                     lhsT_scale=beta_scales[b][:, v * P : (v + 1) * P],
-                    rhs=h_codes[b][:, 2 * P :].bitcast(FP8X4),
-                    rhs_scale=h_scales[b][:, 2 * P :],
+                    rhs=h_codes[b][:, HALF:].bitcast(FP8X4),
+                    rhs_scale=h_scales[b][:, HALF:],
                     start=True,
                     stop=True,
                 )
@@ -254,6 +259,14 @@ def tile_transformer_pa_t_kernel(tc, x, f, g, mask, Wv, gamma, out):
                     stop=True,
                 )
 
+        def result_tile(b):
+            if b not in result:
+                result[b] = work.tile([P, PACK, N], F32, name="result", tag="result", bufs=3)
+            return result[b]
+
+        def store(b, u):
+            nc.sync.dma_start(out=out[b][u * P : (u + 1) * P, :], in_=result[b][:, u, :])
+
         def scale_o(b, u):
             if u == 0:
                 scaled[b] = work.tile([P, 2, N], F32, name="scaled", tag="scaled")
@@ -266,29 +279,21 @@ def tile_transformer_pa_t_kernel(tc, x, f, g, mask, Wv, gamma, out):
                 op1=ALU.mult,
             )
 
+        def add_x(engine, b, u):
+            engine.tensor_tensor(
+                out=result_tile(b)[:, u, :], in0=scaled[b][:, u, :], in1=x_rows[b][:, u, :], op=ALU.add
+            )
+            store(b, u)
+
         def scale_ot(b, v):
             if v == 0:
-                scaled_t[b] = work.tile([P, PACK, 2 * P], F32, name="scaled_t", tag="scaled_t")
+                scaled_t[b] = work.tile([P, PACK, HALF], F32, name="scaled_t", tag="scaled_t")
             nc.scalar.activation(
                 out=scaled_t[b][:, v, :],
                 in_=ot_ps[b, v // 2][:, v % 2, :],
                 func=ACT.Copy,
                 scale=gamma_mask_cols[:, PACK * b + v : PACK * b + v + 1],
             )
-
-        def result_tile(b):
-            if b not in result:
-                result[b] = work.tile([P, PACK, N], F32, name="result", tag="result", bufs=3)
-            return result[b]
-
-        def store(b, u):
-            nc.sync.dma_start(out=out[b][u * P : (u + 1) * P, :], in_=result[b][:, u, :])
-
-        def add_x(engine, b, u):
-            engine.tensor_tensor(
-                out=result_tile(b)[:, u, :], in0=scaled[b][:, u, :], in1=x_rows[b][:, u, :], op=ALU.add
-            )
-            store(b, u)
 
         def put_x(b, u):
             sum_ps[b, u] = psum.tile([P, N], F32, name="sum_ps", tag="h_or_beta", bufs=3)
@@ -305,14 +310,22 @@ def tile_transformer_pa_t_kernel(tc, x, f, g, mask, Wv, gamma, out):
                     stop=v == PACK - 1,
                 )
 
-        def add_x_in_psum(b, u):
-            put_x(b, u)
-            add_scaled(b, u)
-
         def copy_sum(engine, b, u):
-            copy = nc.scalar.copy if engine == SCALAR else nc.vector.tensor_copy
-            copy(out=result_tile(b)[:, u, :], in_=sum_ps[b, u][:])
+            copy(engine, result_tile(b)[:, u, :], sum_ps[b, u][:])
             store(b, u)
+
+        def keep_clock(b, n):
+            unread = psum.tile([P, N], F32, name="unread", tag="mask", bufs=1)
+            for _ in range(n):
+                nc.tensor.matmul_mx(
+                    out=unread[:],
+                    lhsT=w_codes[:, :P].bitcast(FP8X4),
+                    lhsT_scale=w_scales[:, :P],
+                    rhs=h_codes[b][:].bitcast(FP8X4),
+                    rhs_scale=h_scales[b][:],
+                    start=True,
+                    stop=True,
+                )
 
         def on(b):
             return 0 <= b < B
@@ -329,18 +342,18 @@ def tile_transformer_pa_t_kernel(tc, x, f, g, mask, Wv, gamma, out):
                 in_=mask.rearrange("b (t p) -> (b t) p", p=P),
             )
         load(1)
+        load(2)
         mask_rows = const.tile([P, B, N], BF16)
         nc.sync.dma_start(
             out=mask_rows[:].rearrange("p b n -> p (b n)"), in_=mask.rearrange("b n -> (b n)").partition_broadcast(P)
         )
-        load(2)
         identity_bf = const.tile([P, P], BF16)
         make_identity(nc, identity_bf[:])
         identity = const.tile([P, P], F32)
         make_identity(nc, identity[:])
 
-        for q in range(PACK):
-            scores(0, q)
+        for v in range(PACK):
+            scores(0, v)
         for v in range(PACK):
             maximum(0, v)
         for v in range(PACK):
@@ -349,8 +362,10 @@ def tile_transformer_pa_t_kernel(tc, x, f, g, mask, Wv, gamma, out):
 
         gamma_col = const.tile([P, 1], F32)
         nc.vector.tensor_copy(out=gamma_col[:], in_=gamma_bf[:])
-        regroup_x(SCALAR, 0, 0, 320)
-        regroup_x(GPSIMD, 0, 320, N)
+
+        regroup_x(SCALAR, 0, 0, HALF)
+        regroup_x(GPSIMD, 0, HALF, N)
+
         w_grouped = const.tile([P, C, PACK], BF16, align_bytes=64)
         for u in range(PACK):
             w_t = psum.tile([P, PACK, P], BF16, name="w_t", tag="h_or_beta", bufs=3)
@@ -361,13 +376,16 @@ def tile_transformer_pa_t_kernel(tc, x, f, g, mask, Wv, gamma, out):
         w_scales = const.tile([P, C], U8, align_bytes=64)
         quantise_x(0)
         quantise(nc, w_grouped, w_codes, w_scales)
-        for q in range(PACK):
-            scores(1, q)
-        regroup_x(GPSIMD, 1, 256, N)
-        regroup_x(SCALAR, 1, 0, 256)
-        quantise_x(1)
+
+        for v in range(PACK):
+            scores(1, v)
+        for u in range(3):
+            project(0, u)
+        regroup_x(GPSIMD, 1, HALF, N)
+        regroup_x(SCALAR, 1, 0, HALF)
         for v in range(PACK):
             exponential(0, v)
+
         mask_t = psum.tile([P, P], BF16, name="mask_t", tag="mask", bufs=1)
         nc.tensor.transpose(mask_t[:], mask_tiles[:], identity_bf[:])
         mask_cols = const.tile([P, B * PACK], F32)
@@ -378,33 +396,29 @@ def tile_transformer_pa_t_kernel(tc, x, f, g, mask, Wv, gamma, out):
         )
         spread_mask(0)
 
-        project(0, 0)
-        project(0, 1)
-        project(0, 2)
         for r in range(B - 1):
             if on(r + 3):
                 load(r + 3)
-            copy_h(SCALAR, r, 0)
+            copy_h(r, 0)
             project(r, 3)
-            copy_h(SCALAR, r, 1)
-            copy_h(SCALAR, r, 2)
-            copy_h(SCALAR, r, 3)
+            for u in range(1, PACK):
+                copy_h(r, u)
             if r == 0:
                 for v in range(PACK):
                     maximum(1, v)
+                quantise_x(1)
             if on(r - 2):
                 quantise_beta(r - 2)
                 attend(r - 2)
-            if r > 0:
+            if on(r - 1):
                 quantise_x(r + 1)
-            if r > 0:
-                mask_and_sum(r - 1, 0)
+                mask_and_sum(r - 1, 0, mask_ps[r - 1][:])
             if on(r + 2):
-                regroup_x(GPSIMD, r + 2, 0, 152)
-                regroup_x(GPSIMD, r + 2, 152, 304)
-            if r > 0:
+                regroup_x(GPSIMD, r + 2, 0, X_COLS_FIRST // 2)
+                regroup_x(GPSIMD, r + 2, X_COLS_FIRST // 2, X_COLS_FIRST)
+            if on(r - 1):
                 for v in range(1, PACK):
-                    mask_and_sum(r - 1, v)
+                    mask_and_sum(r - 1, v, mask_ps[r - 1][:])
                 quantise_h(r - 1)
                 denominator(r - 1)
             if on(r - 2):
@@ -414,46 +428,42 @@ def tile_transformer_pa_t_kernel(tc, x, f, g, mask, Wv, gamma, out):
                         scores(r + 1, v // 2)
                 put_x(r - 2, 2)
                 put_x(r - 2, 3)
-                add_scaled(r - 2, 2)
-                add_scaled(r - 2, 3)
-                spread_mask(r)
                 scale_o(r - 2, 0)
                 scores(r + 1, 2)
             elif r == 1:
-                spread_mask(r)
-                for q in range(PACK):
-                    scores(r + 1, q)
-            if r > 0:
+                for v in range(PACK):
+                    scores(r + 1, v)
+            if on(r - 1):
                 reciprocal(r - 1)
             if on(r - 2):
                 scale_o(r - 2, 1)
                 scores(r + 1, 3)
-            if r > 0:
+                add_scaled(r - 2, 2)
+                add_scaled(r - 2, 3)
+            if on(r - 1):
+                spread_mask(r)
                 for v in range(3):
                     exponential(r, v)
-                for v in range(3, PACK):
-                    normalise(GPSIMD, r - 1, v)
+                normalise(GPSIMD, r - 1, 3)
             if on(r - 2):
                 add_x(nc.gpsimd, r - 2, 0)
                 add_x(nc.gpsimd, r - 2, 1)
-            if r > 0:
+            if on(r - 1):
                 for v in range(3):
                     normalise(SCALAR, r - 1, v)
                 transpose_beta(r - 1, 0)
                 transpose_beta(r - 1, 1)
             if on(r - 2):
                 copy_sum(SCALAR, r - 2, 2)
-            if r > 0:
+            if on(r - 1):
                 transpose_beta(r - 1, 2)
                 transpose_beta(r - 1, 3)
             if on(r - 2):
                 copy_sum(SCALAR, r - 2, 3)
-            if r > 0:
-                for v in range(3, PACK):
-                    exponential(r, v)
             if on(r + 2):
-                regroup_x(GPSIMD, r + 2, 304, 512)
-            if r > 0:
+                regroup_x(GPSIMD, r + 2, X_COLS_FIRST, N)
+            if on(r - 1):
+                exponential(r, 3)
                 regroup_beta(SCALAR, r - 1, 0)
                 regroup_beta(SCALAR, r - 1, 1)
                 for v in range(PACK):
@@ -464,93 +474,75 @@ def tile_transformer_pa_t_kernel(tc, x, f, g, mask, Wv, gamma, out):
                 leaky(r + 1, v)
             top(r + 1)
 
-        w, z, y = B - 3, B - 2, B - 1
-        copy_h(SCALAR, y, 0)
-        project(y, 3)
-        quantise_beta(w)
-        attend(w)
-        mask_and_sum(z, 0)
-        mask_and_sum(z, 1)
-        mask_and_sum(z, 2)
-        mask_and_sum(z, 3)
-        exponential(y, 0)
-        exponential(y, 1)
-        exponential(y, 2)
-        exponential(y, 3)
-        copy_h(SCALAR, y, 1)
-        copy_h(SCALAR, y, 2)
-        denominator(z)
-        quantise_h(z)
-        scale_ot(w, 0)
-        scale_ot(w, 1)
-        scale_ot(w, 2)
-        scale_ot(w, 3)
-        scale_o(w, 0)
-        reciprocal(z)
-        scale_o(w, 1)
-        put_x(w, 2)
-        put_x(w, 3)
-        add_scaled(w, 2)
-        add_scaled(w, 3)
-        copy_h(SCALAR, y, 3)
-        copy_sum(SCALAR, w, 2)
-        normalise(VECTOR, z, 0)
-        transpose_beta(z, 0)
-        normalise(VECTOR, z, 1)
-        transpose_beta(z, 1)
-        normalise(VECTOR, z, 2)
-        transpose_beta(z, 2)
-        normalise(VECTOR, z, 3)
-        transpose_beta(z, 3)
-        regroup_beta(SCALAR, z, 0)
-        regroup_beta(SCALAR, z, 1)
-        copy_sum(SCALAR, w, 3)
-        mask_and_sum(y, 0)
-        mask_and_sum(y, 1)
-        mask_and_sum(y, 2)
-        mask_and_sum(y, 3)
-        quantise_beta(z)
-        attend(z)
-        denominator(y)
-        quantise_h(y)
-        reciprocal(y)
-        normalise(VECTOR, y, 0)
-        transpose_beta(y, 0)
-        normalise(VECTOR, y, 1)
-        transpose_beta(y, 1)
-        normalise(VECTOR, y, 2)
-        transpose_beta(y, 2)
-        normalise(VECTOR, y, 3)
-        transpose_beta(y, 3)
-        scale_o(z, 0)
-        scale_o(z, 1)
-        scale_ot(z, 0)
-        scale_ot(z, 1)
-        scale_ot(z, 2)
-        scale_ot(z, 3)
-        regroup_beta(SCALAR, y, 0)
-        regroup_beta(VECTOR, y, 1)
-        put_x(z, 2)
-        put_x(z, 3)
-        add_scaled(z, 2)
-        add_scaled(z, 3)
-        quantise_beta(y)
-        attend(y)
-        add_x(nc.vector, w, 0)
-        add_x(nc.vector, w, 1)
-        copy_sum(SCALAR, z, 2)
-        scale_ot(y, 0)
-        scale_ot(y, 1)
-        scale_ot(y, 2)
-        scale_ot(y, 3)
-        scale_o(y, 0)
-        scale_o(y, 1)
-        add_x(nc.gpsimd, z, 0)
-        add_x(nc.vector, y, 0)
-        add_x(nc.vector, y, 1)
-        add_x_in_psum(y, 2)
-        copy_sum(SCALAR, z, 3)
-        add_x_in_psum(y, 3)
-        add_x(nc.vector, z, 1)
-        copy_sum(SCALAR, y, 2)
-        copy_sum(VECTOR, y, 3)
+        i, j, k = B - 3, B - 2, B - 1
+        copy_h(k, 0)
+        project(k, 3)
+        quantise_beta(i)
+        attend(i)
+        for v in range(PACK):
+            mask_and_sum(j, v, mask_ps[j][:])
+        for v in range(PACK):
+            exponential(k, v)
+        copy_h(k, 1)
+        copy_h(k, 2)
+        denominator(j)
+        quantise_h(j)
+        for v in range(PACK):
+            scale_ot(i, v)
+        scale_o(i, 0)
+        reciprocal(j)
+        scale_o(i, 1)
+        for u in (2, 3):
+            put_x(i, u)
+        for u in (2, 3):
+            add_scaled(i, u)
+        copy_h(k, 3)
+        copy_sum(SCALAR, i, 2)
+        for v in range(PACK):
+            normalise(VECTOR, j, v)
+            transpose_beta(j, v)
+        regroup_beta(SCALAR, j, 0)
+        regroup_beta(SCALAR, j, 1)
+        copy_sum(SCALAR, i, 3)
+        for v in range(PACK):
+            mask_and_sum(k, v, mask_rows[:, k, :])
+        keep_clock(j, 3)
+        quantise_beta(j)
+        attend(j)
+        denominator(k)
+        quantise_h(k)
+        reciprocal(k)
+        for v in range(PACK):
+            normalise(VECTOR, k, v)
+            transpose_beta(k, v)
+        scale_o(j, 0)
+        scale_o(j, 1)
+        for v in range(PACK):
+            scale_ot(j, v)
+        regroup_beta(SCALAR, k, 0)
+        regroup_beta(VECTOR, k, 1)
+        keep_clock(j, 3)
+        quantise_beta(k)
+        attend(k)
+        add_x(nc.vector, i, 0)
+        add_x(nc.vector, i, 1)
+        for v in range(PACK):
+            scale_ot(k, v)
+        for u in (2, 3):
+            put_x(j, u)
+        for u in (2, 3):
+            add_scaled(j, u)
+        scale_o(k, 0)
+        scale_o(k, 1)
+        add_x(nc.gpsimd, j, 0)
+        add_x(nc.vector, k, 0)
+        add_x(nc.vector, k, 1)
+        put_x(k, 2)
+        add_scaled(k, 2)
+        copy_sum(SCALAR, j, 2)
+        copy_sum(SCALAR, j, 3)
+        put_x(k, 3)
+        add_scaled(k, 3)
+        add_x(nc.vector, j, 1)
+        copy_sum(SCALAR, k, 2)
+        copy_sum(VECTOR, k, 3)

from contextlib import ExitStack

import concourse.mybir as mybir
from concourse.masks import make_identity

F32 = mybir.dt.float32
BF16 = mybir.dt.bfloat16
U32 = mybir.dt.uint32
U8 = mybir.dt.uint8
FP8X4 = mybir.dt.float8_e4m3fn_x4
ALU = mybir.AluOpType
ACT = mybir.ActivationFunctionType

B, C, CQ, N = 16, 512, 128, 512
P = 128
PACK = 4
HALF = 256
EPS = 1e-6
LEAKY_SLOPE = 0.2
X_COLS_FIRST = 288
SCALAR, VECTOR, GPSIMD = "scalar", "vector", "gpsimd"

FLOPS = B * (2 * C * C * N + 2 * CQ * N * N + 2 * C * N * N)


def quantise(nc, grouped, codes, scales):
    nc.vector.quantize_mx(
        out=codes[:].bitcast(FP8X4),
        scales=scales[:],
        in_=grouped[:].rearrange("p w t -> p (w t)"),
    )


def tile_transformer_pa_t_kernel(tc, x, f, g, mask, Wv, gamma, out):
    nc = tc.nc
    with ExitStack() as stack:
        stack.enter_context(tc.manual_schedule())
        const = stack.enter_context(tc.tile_pool(name="const", bufs=1))
        loads = stack.enter_context(tc.tile_pool(name="loads", bufs=3))
        work = stack.enter_context(tc.tile_pool(name="work", bufs=2))
        stats = stack.enter_context(tc.tile_pool(name="stats", bufs=3))
        psum = stack.enter_context(tc.psum_pool(name="psum", bufs=1))

        x_rows, f_sb, g_sb = {}, {}, {}
        x_grouped, x_codes, x_scales = {}, {}, {}
        h_ps, h_grouped, h_codes, h_scales = {}, {}, {}, {}
        s_ps, neg_leaky, neg_s_max, neg_top = {}, {}, {}, {}
        e_sb, e_sum, mask_ps, em_sum, denom, recip = {}, {}, {}, {}, {}, {}
        beta_t, beta_ps, beta_grouped, beta_codes, beta_scales = {}, {}, {}, {}, {}
        o_ps, ot_ps, scaled, scaled_t, sum_ps, result = {}, {}, {}, {}, {}, {}

        def copy(engine, out, in_):
            if engine == SCALAR:
                nc.scalar.copy(out=out, in_=in_)
            else:
                nc.vector.tensor_copy(out=out, in_=in_)

        def load(b):
            f_sb[b] = loads.tile([P, N], BF16, name="f_sb", tag="f_sb")
            nc.sync.dma_start(out=f_sb[b][:], in_=f[b])
            g_sb[b] = loads.tile([P, N], BF16, name="g_sb", tag="g_sb")
            nc.sync.dma_start(out=g_sb[b][:], in_=g[b])
            x_rows[b] = loads.tile([P, PACK, N], BF16, name="x_rows", tag="x_rows", bufs=6)
            nc.sync.dma_start(out=x_rows[b][:], in_=x[b].rearrange("(t p) n -> p t n", p=P))

        def regroup_x(engine, b, first, last):
            if b not in x_grouped:
                tag = "x_grouped_1" if b == 1 else "x_grouped"
                x_grouped[b] = work.tile([P, N, PACK], BF16, name="x_grouped", tag=tag, bufs=1, align_bytes=64)
            if engine == SCALAR:
                nc.scalar.copy(
                    out=x_grouped[b][:, first:last, :].rearrange("p (c i) t -> p c t i", i=4),
                    in_=x_rows[b][:, :, first:last].rearrange("p t (c i) -> p c t i", i=4),
                )
            else:
                nc.gpsimd.tensor_scalar(
                    out=x_grouped[b][:, first:last, :],
                    in0=x_rows[b][:, :, first:last].rearrange("p t c -> p c t"),
                    scalar1=1.0,
                    scalar2=0.0,
                    op0=ALU.mult,
                    op1=ALU.add,
                )

        def quantise_x(b):
            x_codes[b] = work.tile([P, N], U32, name="x_codes", tag="x_codes", align_bytes=64)
            x_scales[b] = work.tile([P, N], U8, name="x_scales", tag="x_scales", align_bytes=64)
            quantise(nc, x_grouped[b], x_codes[b], x_scales[b])

        def project(b, u):
            h_ps[b, u] = psum.tile([P, PACK, P], F32, name="h_ps", tag="h_or_beta", bufs=3)
            for t in range(PACK):
                nc.tensor.matmul_mx(
                    out=h_ps[b, u][:, t, :],
                    lhsT=x_codes[b][:, t * P : (t + 1) * P].bitcast(FP8X4),
                    lhsT_scale=x_scales[b][:, t * P : (t + 1) * P],
                    rhs=w_codes[:, u * P : (u + 1) * P].bitcast(FP8X4),
                    rhs_scale=w_scales[:, u * P : (u + 1) * P],
                    start=True,
                    stop=True,
                )

        def copy_h(b, u):
            if u == 0:
                h_grouped[b] = work.tile([P, N, PACK], BF16, name="h_grouped", tag="h_grouped", align_bytes=64)
            nc.scalar.copy(
                out=h_grouped[b][:, u * P : (u + 1) * P, :], in_=h_ps[b, u][:].rearrange("p t o -> p o t")
            )

        def quantise_h(b):
            h_codes[b] = work.tile([P, N], U32, name="h_codes", tag="h_codes", align_bytes=64)
            h_scales[b] = work.tile([P, N], U8, name="h_scales", tag="h_scales", align_bytes=64)
            quantise(nc, h_grouped[b], h_codes[b], h_scales[b])

        def scores(b, v):
            s_ps[b, v] = psum.tile([P, N], F32, name="s_ps", tag="s_or_o", bufs=4)
            nc.tensor.matmul(
                out=s_ps[b, v][:], lhsT=g_sb[b][:, v * P : (v + 1) * P], rhs=f_sb[b][:], start=True, stop=True
            )

        def maximum(b, v):
            if v == 0:
                neg_leaky[b] = work.tile([P, PACK, N], F32, name="neg_leaky", tag="neg_leaky")
                neg_s_max[b] = stats.tile([P, PACK], F32, name="neg_s_max", tag="neg_s_max")
            nc.vector.tensor_scalar(
                out=neg_leaky[b][:, v, :],
                in0=s_ps[b, v][:],
                scalar1=-1.0,
                scalar2=None,
                op0=ALU.mult,
                op1=ALU.min,
                accum_out=neg_s_max[b][:, v : v + 1],
            )

        def leaky(b, v):
            nc.vector.scalar_tensor_tensor(
                out=neg_leaky[b][:, v, :],
                in0=s_ps[b, v][:],
                scalar=-LEAKY_SLOPE,
                in1=neg_leaky[b][:, v, :],
                op0=ALU.mult,
                op1=ALU.min,
            )

        def top(b):
            neg_top[b] = stats.tile([P, PACK], F32, name="neg_top", tag="neg_top")
            nc.vector.scalar_tensor_tensor(
                out=neg_top[b][:],
                in0=neg_s_max[b][:],
                scalar=LEAKY_SLOPE,
                in1=neg_s_max[b][:],
                op0=ALU.mult,
                op1=ALU.min,
            )

        def exponential(b, v):
            if v == 0:
                e_sb[b] = work.tile([P, PACK, N], F32, name="e_sb", tag="e_sb")
                e_sum[b] = stats.tile([P, PACK], F32, name="e_sum", tag="e_sum")
            nc.scalar.activation(
                out=e_sb[b][:, v, :],
                in_=neg_leaky[b][:, v, :],
                func=ACT.Exp,
                bias=neg_top[b][:, v : v + 1],
                scale=-1.0,
                accum_out=e_sum[b][:, v : v + 1],
            )

        def spread_mask(b):
            mask_ps[b] = psum.tile([P, N], F32, name="mask_ps", tag="mask", bufs=1)
            for t in range(PACK):
                column = mask_cols[:, PACK * b + t : PACK * b + t + 1]
                nc.tensor.transpose(mask_ps[b][:, t * P : (t + 1) * P], column.to_broadcast([P, P]), identity[:])

        def mask_and_sum(b, v, mask_row):
            if v == 0:
                em_sum[b] = stats.tile([P, PACK], F32, name="em_sum", tag="em_sum")
            nc.vector.scalar_tensor_tensor(
                out=e_sb[b][:, v, :],
                in0=e_sb[b][:, v, :],
                scalar=1.0,
                in1=mask_row,
                op0=ALU.mult,
                op1=ALU.mult,
                accum_out=em_sum[b][:, v : v + 1],
            )

        def denominator(b):
            denom[b] = stats.tile([P, PACK], F32, name="denom", tag="denom")
            nc.vector.scalar_tensor_tensor(
                out=denom[b][:], in0=e_sum[b][:], scalar=EPS, in1=em_sum[b][:], op0=ALU.mult, op1=ALU.add
            )

        def reciprocal(b):
            recip[b] = stats.tile([P, PACK], F32, name="recip", tag="recip")
            nc.vector.reciprocal(out=recip[b][:], in_=denom[b][:])

        def normalise(engine, b, v):
            if b not in beta_t:
                beta_t[b] = work.tile([P, PACK, N], BF16, name="beta_t", tag="beta_t")
            pairs = beta_t[b][:, v, :].rearrange("p (u q e) -> p u q e", u=2, e=2)
            em = e_sb[b][:, v, :].rearrange("p (u e q) -> p u q e", u=2, e=2)
            factor = recip[b][:, v : v + 1]
            if engine == SCALAR:
                nc.scalar.activation(out=pairs, in_=em, func=ACT.Copy, scale=factor)
            elif engine == VECTOR:
                nc.vector.tensor_scalar(out=pairs, in0=em, scalar1=factor, scalar2=None, op0=ALU.mult)
            else:
                nc.gpsimd.tensor_scalar(
                    out=pairs, in0=em, scalar1=factor, scalar2=0.0, op0=ALU.mult, op1=ALU.add
                )

        def transpose_beta(b, v):
            if v % 2 == 0:
                beta_ps[b, v // 2] = psum.tile([P, 2, 2, P], F32, name="beta_ps", tag="h_or_beta", bufs=3)
            words = beta_t[b][:, v, :].bitcast(F32)
            for u in range(2):
                nc.tensor.transpose(beta_ps[b, v // 2][:, v % 2, u, :], words[:, u * P : (u + 1) * P], identity[:])

        def regroup_beta(engine, b, w):
            if w == 0:
                beta_grouped[b] = work.tile(
                    [P, N, PACK], BF16, name="beta_grouped", tag="beta_grouped", align_bytes=64
                )
            words = beta_grouped[b][:, w * 2 * P : (w + 1) * 2 * P, :].rearrange("p n t -> p (n t)").bitcast(F32)
            copy(
                engine,
                words.rearrange("p (v j u) -> p v j u", v=2, u=2),
                beta_ps[b, w][:].rearrange("p v u j -> p v j u"),
            )

        def quantise_beta(b):
            beta_codes[b] = work.tile([P, N], U32, name="beta_codes", tag="beta_codes", align_bytes=64)
            beta_scales[b] = work.tile([P, N], U8, name="beta_scales", tag="beta_scales", align_bytes=64)
            quantise(nc, beta_grouped[b], beta_codes[b], beta_scales[b])

        def attend(b):
            for v in range(PACK):
                if v % 2 == 0:
                    ot_ps[b, v // 2] = psum.tile([P, 2, HALF], F32, name="ot_ps", tag="s_or_o", bufs=4)
                nc.tensor.matmul_mx(
                    out=ot_ps[b, v // 2][:, v % 2, :],
                    lhsT=beta_codes[b][:, v * P : (v + 1) * P].bitcast(FP8X4),
                    lhsT_scale=beta_scales[b][:, v * P : (v + 1) * P],
                    rhs=h_codes[b][:, HALF:].bitcast(FP8X4),
                    rhs_scale=h_scales[b][:, HALF:],
                    start=True,
                    stop=True,
                )
            for u in range(2):
                o_ps[b, u] = psum.tile([P, N], F32, name="o_ps", tag="s_or_o", bufs=4)
                nc.tensor.matmul_mx(
                    out=o_ps[b, u][:],
                    lhsT=h_codes[b][:, u * P : (u + 1) * P].bitcast(FP8X4),
                    lhsT_scale=h_scales[b][:, u * P : (u + 1) * P],
                    rhs=beta_codes[b][:].bitcast(FP8X4),
                    rhs_scale=beta_scales[b][:],
                    start=True,
                    stop=True,
                )

        def result_tile(b):
            if b not in result:
                result[b] = work.tile([P, PACK, N], F32, name="result", tag="result", bufs=3)
            return result[b]

        def store(b, u):
            nc.sync.dma_start(out=out[b][u * P : (u + 1) * P, :], in_=result[b][:, u, :])

        def scale_o(b, u):
            if u == 0:
                scaled[b] = work.tile([P, 2, N], F32, name="scaled", tag="scaled")
            nc.vector.scalar_tensor_tensor(
                out=scaled[b][:, u, :],
                in0=o_ps[b, u][:],
                scalar=gamma_col[:, 0:1],
                in1=mask_rows[:, b, :],
                op0=ALU.mult,
                op1=ALU.mult,
            )

        def add_x(engine, b, u):
            engine.tensor_tensor(
                out=result_tile(b)[:, u, :], in0=scaled[b][:, u, :], in1=x_rows[b][:, u, :], op=ALU.add
            )
            store(b, u)

        def scale_ot(b, v):
            if v == 0:
                scaled_t[b] = work.tile([P, PACK, HALF], F32, name="scaled_t", tag="scaled_t")
            nc.scalar.activation(
                out=scaled_t[b][:, v, :],
                in_=ot_ps[b, v // 2][:, v % 2, :],
                func=ACT.Copy,
                scale=gamma_mask_cols[:, PACK * b + v : PACK * b + v + 1],
            )

        def put_x(b, u):
            sum_ps[b, u] = psum.tile([P, N], F32, name="sum_ps", tag="h_or_beta", bufs=3)
            nc.tensor.matmul(out=sum_ps[b, u][:], lhsT=identity_bf[:], rhs=x_rows[b][:, u, :], start=True, stop=False)

        def add_scaled(b, u):
            for v in range(PACK):
                nc.tensor.matmul(
                    out=sum_ps[b, u][:, v * P : (v + 1) * P],
                    lhsT=scaled_t[b][:, v, (u - 2) * P : (u - 1) * P],
                    rhs=identity[:],
                    is_transpose=True,
                    start=False,
                    stop=v == PACK - 1,
                )

        def copy_sum(engine, b, u):
            copy(engine, result_tile(b)[:, u, :], sum_ps[b, u][:])
            store(b, u)

        def keep_clock(b, n):
            unread = psum.tile([P, N], F32, name="unread", tag="mask", bufs=1)
            for _ in range(n):
                nc.tensor.matmul_mx(
                    out=unread[:],
                    lhsT=w_codes[:, :P].bitcast(FP8X4),
                    lhsT_scale=w_scales[:, :P],
                    rhs=h_codes[b][:].bitcast(FP8X4),
                    rhs_scale=h_scales[b][:],
                    start=True,
                    stop=True,
                )

        def on(b):
            return 0 <= b < B

        load(0)
        w_rows = const.tile([P, PACK, C], BF16)
        nc.sync.dma_start(out=w_rows[:], in_=Wv.rearrange("(u p) c -> p u c", p=P))
        gamma_bf = const.tile([P, 1], BF16)
        nc.sync.dma_start(out=gamma_bf[:], in_=gamma.partition_broadcast(P))
        mask_tiles = const.tile([P, P], BF16)
        for half in range(2):
            nc.sync.dma_start(
                out=mask_tiles[half * B * PACK : (half + 1) * B * PACK, :],
                in_=mask.rearrange("b (t p) -> (b t) p", p=P),
            )
        load(1)
        load(2)
        mask_rows = const.tile([P, B, N], BF16)
        nc.sync.dma_start(
            out=mask_rows[:].rearrange("p b n -> p (b n)"), in_=mask.rearrange("b n -> (b n)").partition_broadcast(P)
        )
        identity_bf = const.tile([P, P], BF16)
        make_identity(nc, identity_bf[:])
        identity = const.tile([P, P], F32)
        make_identity(nc, identity[:])

        for v in range(PACK):
            scores(0, v)
        for v in range(PACK):
            maximum(0, v)
        for v in range(PACK):
            leaky(0, v)
        top(0)

        gamma_col = const.tile([P, 1], F32)
        nc.vector.tensor_copy(out=gamma_col[:], in_=gamma_bf[:])

        regroup_x(SCALAR, 0, 0, HALF)
        regroup_x(GPSIMD, 0, HALF, N)

        w_grouped = const.tile([P, C, PACK], BF16, align_bytes=64)
        for u in range(PACK):
            w_t = psum.tile([P, PACK, P], BF16, name="w_t", tag="h_or_beta", bufs=3)
            for t in range(PACK):
                nc.tensor.transpose(w_t[:, t, :], w_rows[:, u, t * P : (t + 1) * P], identity_bf[:])
            nc.scalar.copy(out=w_grouped[:, u * P : (u + 1) * P, :], in_=w_t[:].rearrange("p t o -> p o t"))
        w_codes = const.tile([P, C], U32, align_bytes=64)
        w_scales = const.tile([P, C], U8, align_bytes=64)
        quantise_x(0)
        quantise(nc, w_grouped, w_codes, w_scales)

        for v in range(PACK):
            scores(1, v)
        for u in range(3):
            project(0, u)
        regroup_x(GPSIMD, 1, HALF, N)
        regroup_x(SCALAR, 1, 0, HALF)
        for v in range(PACK):
            exponential(0, v)

        mask_t = psum.tile([P, P], BF16, name="mask_t", tag="mask", bufs=1)
        nc.tensor.transpose(mask_t[:], mask_tiles[:], identity_bf[:])
        mask_cols = const.tile([P, B * PACK], F32)
        nc.scalar.copy(out=mask_cols[:], in_=mask_t[:, : B * PACK])
        gamma_mask_cols = const.tile([P, B * PACK], F32)
        nc.scalar.activation(
            out=gamma_mask_cols[:], in_=mask_t[:, : B * PACK], func=ACT.Copy, scale=gamma_col[:, 0:1]
        )
        spread_mask(0)

        for r in range(B - 1):
            if on(r + 3):
                load(r + 3)
            copy_h(r, 0)
            project(r, 3)
            for u in range(1, PACK):
                copy_h(r, u)
            if r == 0:
                for v in range(PACK):
                    maximum(1, v)
                quantise_x(1)
            if on(r - 2):
                quantise_beta(r - 2)
                attend(r - 2)
            if on(r - 1):
                quantise_x(r + 1)
                mask_and_sum(r - 1, 0, mask_ps[r - 1][:])
            if on(r + 2):
                regroup_x(GPSIMD, r + 2, 0, X_COLS_FIRST // 2)
                regroup_x(GPSIMD, r + 2, X_COLS_FIRST // 2, X_COLS_FIRST)
            if on(r - 1):
                for v in range(1, PACK):
                    mask_and_sum(r - 1, v, mask_ps[r - 1][:])
                quantise_h(r - 1)
                denominator(r - 1)
            if on(r - 2):
                for v in range(PACK):
                    scale_ot(r - 2, v)
                    if v % 2 == 1:
                        scores(r + 1, v // 2)
                put_x(r - 2, 2)
                put_x(r - 2, 3)
                scale_o(r - 2, 0)
                scores(r + 1, 2)
            elif r == 1:
                for v in range(PACK):
                    scores(r + 1, v)
            if on(r - 1):
                reciprocal(r - 1)
            if on(r - 2):
                scale_o(r - 2, 1)
                scores(r + 1, 3)
                add_scaled(r - 2, 2)
                add_scaled(r - 2, 3)
            if on(r - 1):
                spread_mask(r)
                for v in range(3):
                    exponential(r, v)
                normalise(GPSIMD, r - 1, 3)
            if on(r - 2):
                add_x(nc.gpsimd, r - 2, 0)
                add_x(nc.gpsimd, r - 2, 1)
            if on(r - 1):
                for v in range(3):
                    normalise(SCALAR, r - 1, v)
                transpose_beta(r - 1, 0)
                transpose_beta(r - 1, 1)
            if on(r - 2):
                copy_sum(SCALAR, r - 2, 2)
            if on(r - 1):
                transpose_beta(r - 1, 2)
                transpose_beta(r - 1, 3)
            if on(r - 2):
                copy_sum(SCALAR, r - 2, 3)
            if on(r + 2):
                regroup_x(GPSIMD, r + 2, X_COLS_FIRST, N)
            if on(r - 1):
                exponential(r, 3)
                regroup_beta(SCALAR, r - 1, 0)
                regroup_beta(SCALAR, r - 1, 1)
                for v in range(PACK):
                    maximum(r + 1, v)
            for u in range(3):
                project(r + 1, u)
            for v in range(PACK):
                leaky(r + 1, v)
            top(r + 1)

        i, j, k = B - 3, B - 2, B - 1
        copy_h(k, 0)
        project(k, 3)
        quantise_beta(i)
        attend(i)
        for v in range(PACK):
            mask_and_sum(j, v, mask_ps[j][:])
        for v in range(PACK):
            exponential(k, v)
        copy_h(k, 1)
        copy_h(k, 2)
        denominator(j)
        quantise_h(j)
        for v in range(PACK):
            scale_ot(i, v)
        scale_o(i, 0)
        reciprocal(j)
        scale_o(i, 1)
        for u in (2, 3):
            put_x(i, u)
        for u in (2, 3):
            add_scaled(i, u)
        copy_h(k, 3)
        copy_sum(SCALAR, i, 2)
        for v in range(PACK):
            normalise(VECTOR, j, v)
            transpose_beta(j, v)
        regroup_beta(SCALAR, j, 0)
        regroup_beta(SCALAR, j, 1)
        copy_sum(SCALAR, i, 3)
        for v in range(PACK):
            mask_and_sum(k, v, mask_rows[:, k, :])
        keep_clock(j, 3)
        quantise_beta(j)
        attend(j)
        denominator(k)
        quantise_h(k)
        reciprocal(k)
        for v in range(PACK):
            normalise(VECTOR, k, v)
            transpose_beta(k, v)
        scale_o(j, 0)
        scale_o(j, 1)
        for v in range(PACK):
            scale_ot(j, v)
        regroup_beta(SCALAR, k, 0)
        regroup_beta(VECTOR, k, 1)
        keep_clock(j, 3)
        quantise_beta(k)
        attend(k)
        add_x(nc.vector, i, 0)
        add_x(nc.vector, i, 1)
        for v in range(PACK):
            scale_ot(k, v)
        for u in (2, 3):
            put_x(j, u)
        for u in (2, 3):
            add_scaled(j, u)
        scale_o(k, 0)
        scale_o(k, 1)
        add_x(nc.gpsimd, j, 0)
        add_x(nc.vector, k, 0)
        add_x(nc.vector, k, 1)
        put_x(k, 2)
        add_scaled(k, 2)
        copy_sum(SCALAR, j, 2)
        copy_sum(SCALAR, j, 3)
        put_x(k, 3)
        add_scaled(k, 3)
        add_x(nc.vector, j, 1)
        copy_sum(SCALAR, k, 2)
        copy_sum(VECTOR, k, 3)
